import numpy as np
import ml_dtypes


def mxq(x, axis, fmt="e4m3"):
    dtype, down = {"e4m3": (ml_dtypes.float8_e4m3fn, 7), "e5m2": (ml_dtypes.float8_e5m2, 14)}[fmt]
    v = np.moveaxis(np.asarray(x, np.float32).astype(ml_dtypes.bfloat16).astype(np.float64), axis, -1)
    blocks = v.reshape(v.shape[:-1] + (-1, 32))
    amax = np.abs(blocks).max(-1, keepdims=True)
    byte = np.maximum(np.where(amax > 0, np.frexp(amax)[1] - 1 + 127, 0) - down, 1)
    scale = np.exp2(byte - 127.0)
    codes = (blocks / scale).astype(np.float32).astype(dtype).astype(np.float64)
    return np.moveaxis((codes * scale).reshape(v.shape), -1, axis)


WIDE = False


def mx_kscale(k):
    if not WIDE:
        return np.ones(k)
    levels = np.array([10, -10, 5, -5, 0])
    a = np.random.permutation(np.resize(levels, k // 512 * 4)).reshape(k // 512, 4)
    idx = np.arange(k)
    return np.exp2(a[idx // 512, idx % 128 // 32])


BF16 = ml_dtypes.bfloat16


def bf(x):
    return np.asarray(x, np.float32).astype(BF16)


def f64(x):
    return np.asarray(x).astype(np.float64)


B, S, H, DK, F = 4, 1024, 8, 64, 1024
D = H * DK
EPS = 1e-14


def layer_norm(u, gamma, beta):
    mean = u.mean(-1, keepdims=True)
    var = np.square(u - mean).mean(-1, keepdims=True)
    return (u - mean) / np.sqrt(var + EPS) * gamma + beta


def setup_inputs():
    r = np.random.standard_normal
    t = mx_kscale(F)
    return {"h": bf(r((B, S, D))),
            "W1": bf(r((D, F)) / np.sqrt(D) * t),
            "b1": bf(0.3 * r(F) * t),
            "W2": bf(r((F, D)) / np.sqrt(F) / t[:, None]),
            "b2": bf(0.3 * r(D)),
            "gamma2": bf(1.0 + 0.1 * r(D)),
            "beta2": bf(0.1 * r(D))}


def reference(h, W1, b1, W2, b2, gamma2, beta2):
    hh = f64(h)
    f = (mxq(hh, 2, "e4m3") @ mxq(f64(W1), 0, "e4m3")) + f64(b1)
    f = (mxq(f, 2, "e4m3") @ mxq(f64(W2), 0, "e4m3")) + f64(b2)
    return layer_norm(hh + f, f64(gamma2), f64(beta2))

@@ -1,0 +1,249 @@
+from contextlib import ExitStack
+
+import concourse.mybir as mybir
+from concourse.masks import make_identity
+
+F32 = mybir.dt.float32
+BF16 = mybir.dt.bfloat16
+U32 = mybir.dt.uint32
+U8 = mybir.dt.uint8
+FP8X4 = mybir.dt.float8_e4m3fn_x4
+ACT = mybir.ActivationFunctionType
+ALU = mybir.AluOpType
+
+P = 128
+PACK = 4
+D = 512
+F = 1024
+TOKENS = 4 * 1024
+SUB = 4
+CHUNK = SUB * P
+N_CHUNKS = TOKENS // CHUNK
+F_TILES = F // P
+PASSES2 = F // (P * PACK)
+EPS = 1e-14
+
+FLOPS = 2 * TOKENS * D * F * 2
+
+
+def regroup(engine_copy, grouped, planes):
+    engine_copy(
+        out=grouped.rearrange("p (c i) t -> p c t i", i=4),
+        in_=planes.rearrange("p t (c i) -> p c t i", i=4),
+    )
+
+
+def gpsimd_copy(nc):
+    def copy(out, in_):
+        nc.gpsimd.tensor_scalar(
+            out=out, in0=in_, scalar1=1.0, scalar2=0.0, op0=ALU.mult, op1=ALU.add
+        )
+
+    return copy
+
+
+def tile_encoderblock_pb_t_kernel(tc, h, W1, b1, W2, b2, gamma2, beta2, out):
+    nc = tc.nc
+    h_chunks = h.flatten_outer_dims().rearrange("(c p i) d -> c p i d", p=P, i=SUB)
+    out_chunks = out.flatten_outer_dims().rearrange("(c p i) d -> c p i d", p=P, i=SUB)
+
+    with ExitStack() as ctx:
+        keep = ctx.enter_context(tc.tile_pool(name="keep", bufs=1))
+        work = ctx.enter_context(tc.tile_pool(name="work", bufs=2))
+        psum = ctx.enter_context(tc.psum_pool(name="psum", bufs=2))
+
+        w1_raw = keep.tile([P, PACK, F], BF16)
+        w1_rows = W1.rearrange("(u q e) f -> u q e f", u=2, e=2)
+        h_all = keep.tile([P, N_CHUNKS, SUB, D], BF16)
+
+        def load_w1_half(half):
+            cols = slice(half * (F // 2), (half + 1) * (F // 2))
+            for u in range(2):
+                nc.sync.dma_start(out=w1_raw[:, 2 * u : 2 * u + 2, cols], in_=w1_rows[u][:, :, cols])
+
+        load_w1_half(0)
+        nc.sync.dma_start(out=h_all[:, 0], in_=h_chunks[0])
+        load_w1_half(1)
+        w2_raw = keep.tile([P, PASSES2, PACK, D], BF16)
+        nc.sync.dma_start(
+            out=w2_raw[:].rearrange("p g t n -> p (g t) n"),
+            in_=W2.rearrange("(m p) n -> p m n", p=P),
+        )
+        for c in range(1, N_CHUNKS):
+            nc.sync.dma_start(out=h_all[:, c], in_=h_chunks[c])
+
+        b1_rows = keep.tile([P, P], BF16)
+        nc.vector.memset(b1_rows[:], 0.0)
+        nc.scalar.dma_start(out=b1_rows[0:F_TILES, :], in_=b1.rearrange("(m p) -> m p", p=P))
+        b2_all = keep.tile([P, D], BF16)
+        nc.scalar.dma_start(out=b2_all[:], in_=b2.partition_broadcast(P))
+        gamma_all = keep.tile([P, D], BF16)
+        nc.scalar.dma_start(out=gamma_all[:], in_=gamma2.partition_broadcast(P))
+        beta_all = keep.tile([P, D], BF16)
+        nc.scalar.dma_start(out=beta_all[:], in_=beta2.partition_broadcast(P))
+
+        identity = keep.tile([P, P], F32)
+        make_identity(nc, identity[:])
+        eps = keep.tile([P, 1], F32)
+        nc.vector.memset(eps[:], EPS)
+
+        b1_rows_f32 = keep.tile([P, P], F32)
+        nc.vector.tensor_copy(out=b1_rows_f32[:], in_=b1_rows[:])
+        b1_turned = psum.tile([P, 2, 2, P], F32, tag="turned")
+        nc.tensor.transpose(b1_turned[:, 0, 0, :], b1_rows_f32[:], identity[:])
+        b1_cols = keep.tile([P, F_TILES], F32)
+        nc.vector.tensor_copy(out=b1_cols[:], in_=b1_turned[:, 0, 0, 0:F_TILES])
+
+        w1_grouped = keep.tile([P, F, PACK], BF16, align_bytes=64)
+        w1_codes = keep.tile([P, F], U32, align_bytes=64)
+        w1_scales = keep.tile([P, F], U8, align_bytes=64)
+        w2_grouped = keep.tile([P, PASSES2, D, PACK], BF16, align_bytes=64)
+        w2_codes = keep.tile([P, PASSES2, D], U32, align_bytes=64)
+        w2_scales = keep.tile([P, PASSES2, D], U8, align_bytes=64)
+        for half, engine_copy in enumerate((nc.vector.tensor_copy, nc.scalar.copy)):
+            cols = slice(half * (F // 2), (half + 1) * (F // 2))
+            regroup(engine_copy, w1_grouped[:, cols, :], w1_raw[:, :, cols])
+        for half in range(2):
+            cols = slice(half * (F // 2), (half + 1) * (F // 2))
+            nc.vector.quantize_mx(
+                out=w1_codes[:, cols].bitcast(FP8X4),
+                scales=w1_scales[:, cols],
+                in_=w1_grouped[:, cols, :].rearrange("p f t -> p (f t)"),
+            )
+        for g in range(PASSES2):
+            regroup(gpsimd_copy(nc), w2_grouped[:, g], w2_raw[:, g])
+        for g in range(PASSES2):
+            nc.vector.quantize_mx(
+                out=w2_codes[:, g, :].bitcast(FP8X4),
+                scales=w2_scales[:, g, :],
+                in_=w2_grouped[:, g].rearrange("p n t -> p (n t)"),
+            )
+
+        h_quantised = {}
+        f1_quantised = {}
+        residuals = {}
+
+        def turn_and_quantise_h(c):
+            h_grouped = work.tile([P, CHUNK, PACK], BF16, align_bytes=64)
+            grouped_words = h_grouped[:].rearrange("p w t -> p (w t)").bitcast(F32)
+            for pair in range(SUB // 2):
+                turned = psum.tile([P, 2, 2, P], F32, tag="turned")
+                for j in range(2):
+                    words = h_all[:, c, 2 * pair + j, :].bitcast(F32)
+                    for u in range(2):
+                        nc.tensor.transpose(
+                            turned[:, j, u, :], words[:, u * P : (u + 1) * P], identity[:]
+                        )
+                nc.scalar.copy(
+                    out=grouped_words[:, pair * 4 * P : (pair + 1) * 4 * P].rearrange(
+                        "p (j r u) -> p j r u", j=2, u=2
+                    ),
+                    in_=turned[:].rearrange("p j u r -> p j r u"),
+                )
+            h_codes = work.tile([P, CHUNK], U32, align_bytes=64)
+            h_scales = work.tile([P, CHUNK], U8, align_bytes=64)
+            nc.vector.quantize_mx(
+                out=h_codes[:].bitcast(FP8X4),
+                scales=h_scales[:],
+                in_=h_grouped[:].rearrange("p w t -> p (w t)"),
+            )
+            h_quantised[c] = (h_codes, h_scales)
+            residual = work.tile([P, SUB, D], F32)
+            nc.gpsimd.tensor_tensor(
+                out=residual[:],
+                in0=h_all[:, c],
+                in1=b2_all[:].unsqueeze(1).to_broadcast([P, SUB, D]),
+                op=ALU.add,
+            )
+            residuals[c] = residual
+
+        def first_matmul(c):
+            h_codes, h_scales = h_quantised.pop(c)
+            f1_planes = work.tile([P, F_TILES, CHUNK], BF16)
+            for m in range(F_TILES):
+                units = slice(m * P, (m + 1) * P)
+                acc1 = psum.tile([P, CHUNK], F32, bufs=3)
+                nc.tensor.matmul_mx(
+                    out=acc1[:],
+                    lhsT=w1_codes[:, units].bitcast(FP8X4),
+                    lhsT_scale=w1_scales[:, units],
+                    rhs=h_codes[:].bitcast(FP8X4),
+                    rhs_scale=h_scales[:],
+                    start=True,
+                    stop=True,
+                )
+                nc.scalar.activation(
+                    out=f1_planes[:, m, :], in_=acc1[:], func=ACT.Identity,
+                    bias=b1_cols[:, m : m + 1], scale=1.0,
+                )
+            f1_grouped = work.tile([P, PASSES2, CHUNK, PACK], BF16, align_bytes=64)
+            f1_codes = work.tile([P, PASSES2, CHUNK], U32, align_bytes=64)
+            f1_scales = work.tile([P, PASSES2, CHUNK], U8, align_bytes=64)
+            for g, engine_copy in enumerate((nc.vector.tensor_copy, nc.scalar.copy)):
+                regroup(engine_copy, f1_grouped[:, g], f1_planes[:, g * PACK : (g + 1) * PACK, :])
+            for g in range(PASSES2):
+                nc.vector.quantize_mx(
+                    out=f1_codes[:, g, :].bitcast(FP8X4),
+                    scales=f1_scales[:, g, :],
+                    in_=f1_grouped[:, g].rearrange("p w t -> p (w t)"),
+                )
+            f1_quantised[c] = (f1_codes, f1_scales)
+
+        def second_matmul_and_norm(c):
+            f1_codes, f1_scales = f1_quantised.pop(c)
+            residual = residuals.pop(c)
+            u = work.tile([P, SUB, D], F32)
+            u_sum = work.tile([P, SUB], F32)
+            for i in range(SUB):
+                tokens = slice(i * P, (i + 1) * P)
+                acc2 = psum.tile([P, D], F32, bufs=3)
+                for g in range(PASSES2):
+                    nc.tensor.matmul_mx(
+                        out=acc2[:],
+                        lhsT=f1_codes[:, g, tokens].bitcast(FP8X4),
+                        lhsT_scale=f1_scales[:, g, tokens],
+                        rhs=w2_codes[:, g, :].bitcast(FP8X4),
+                        rhs_scale=w2_scales[:, g, :],
+                        start=(g == 0),
+                        stop=(g == PASSES2 - 1),
+                    )
+                nc.vector.scalar_tensor_tensor(
+                    out=u[:, i, :], in0=acc2[:], scalar=1.0, in1=residual[:, i, :],
+                    op0=ALU.mult, op1=ALU.add, accum_out=u_sum[:, i : i + 1],
+                )
+            minus_mean = work.tile([P, SUB], F32)
+            nc.vector.tensor_scalar_mul(out=minus_mean[:], in0=u_sum[:], scalar1=-1.0 / D)
+            squares = work.tile([P, SUB, D], BF16)
+            square_sum = work.tile([P, SUB], F32)
+            for i in range(SUB):
+                nc.scalar.activation(
+                    out=squares[:, i, :], in_=u[:, i, :], func=ACT.Square,
+                    bias=minus_mean[:, i : i + 1], scale=1.0, accum_out=square_sum[:, i : i + 1],
+                )
+            deviation = work.tile([P, SUB], F32)
+            nc.scalar.activation(
+                out=deviation[:], in_=square_sum[:], func=ACT.Sqrt, bias=eps[:], scale=1.0 / D
+            )
+            inv_deviation = work.tile([P, SUB], F32)
+            nc.vector.reciprocal(out=inv_deviation[:], in_=deviation[:])
+            result = work.tile([P, SUB, D], F32)
+            for i in range(SUB):
+                scaled = work.tile([P, D], F32, bufs=4)
+                nc.vector.scalar_tensor_tensor(
+                    out=scaled[:], in0=u[:, i, :], scalar=minus_mean[:, i : i + 1], in1=gamma_all[:],
+                    op0=ALU.add, op1=ALU.mult,
+                )
+                nc.vector.scalar_tensor_tensor(
+                    out=result[:, i, :], in0=scaled[:], scalar=inv_deviation[:, i : i + 1],
+                    in1=beta_all[:], op0=ALU.mult, op1=ALU.add,
+                )
+                if i % 2 == 1:
+                    nc.sync.dma_start(out=out_chunks[c][:, i - 1 : i + 1], in_=result[:, i - 1 : i + 1])
+
+        for step in range(N_CHUNKS + 2):
+            if step < N_CHUNKS:
+                turn_and_quantise_h(step)
+            if 1 <= step <= N_CHUNKS:
+                first_matmul(step - 1)
+            if step >= 2:
+                second_matmul_and_norm(step - 2)

@@ -33,15 +33,6 @@ def regroup(engine_copy, grouped, planes):
     )
 
 
-def gpsimd_copy(nc):
-    def copy(out, in_):
-        nc.gpsimd.tensor_scalar(
-            out=out, in0=in_, scalar1=1.0, scalar2=0.0, op0=ALU.mult, op1=ALU.add
-        )
-
-    return copy
-
-
 def tile_encoderblock_pb_t_kernel(tc, h, W1, b1, W2, b2, gamma2, beta2, out):
     nc = tc.nc
     h_chunks = h.flatten_outer_dims().rearrange("(c p i) d -> c p i d", p=P, i=SUB)
@@ -110,8 +101,8 @@ def tile_encoderblock_pb_t_kernel(tc, h, W1, b1, W2, b2, gamma2, beta2, out):
                 scales=w1_scales[:, cols],
                 in_=w1_grouped[:, cols, :].rearrange("p f t -> p (f t)"),
             )
-        for g in range(PASSES2):
-            regroup(gpsimd_copy(nc), w2_grouped[:, g], w2_raw[:, g])
+        for g, engine_copy in enumerate((nc.vector.tensor_copy, nc.scalar.copy)):
+            regroup(engine_copy, w2_grouped[:, g], w2_raw[:, g])
         for g in range(PASSES2):
             nc.vector.quantize_mx(
                 out=w2_codes[:, g, :].bitcast(FP8X4),
@@ -149,7 +140,7 @@ def tile_encoderblock_pb_t_kernel(tc, h, W1, b1, W2, b2, gamma2, beta2, out):
             )
             h_quantised[c] = (h_codes, h_scales)
             residual = work.tile([P, SUB, D], F32)
-            nc.gpsimd.tensor_tensor(
+            nc.vector.tensor_tensor(
                 out=residual[:],
                 in0=h_all[:, c],
                 in1=b2_all[:].unsqueeze(1).to_broadcast([P, SUB, D]),

@@ -22,6 +22,7 @@ N_CHUNKS = TOKENS // CHUNK
 F_TILES = F // P
 PASSES2 = F // (P * PACK)
 EPS = 1e-14
+VECTOR_COLS = 256
 
 FLOPS = 2 * TOKENS * D * F * 2
 
@@ -39,9 +40,11 @@ def tile_encoderblock_pb_t_kernel(tc, h, W1, b1, W2, b2, gamma2, beta2, out):
     out_chunks = out.flatten_outer_dims().rearrange("(c p i) d -> c p i d", p=P, i=SUB)
 
     with ExitStack() as ctx:
+        ctx.enter_context(tc.manual_schedule())
         keep = ctx.enter_context(tc.tile_pool(name="keep", bufs=1))
         work = ctx.enter_context(tc.tile_pool(name="work", bufs=2))
-        psum = ctx.enter_context(tc.psum_pool(name="psum", bufs=2))
+        fixed_banks = ctx.enter_context(tc.psum_pool(name="fixed_banks", bufs=1))
+        banks = ctx.enter_context(tc.psum_pool(name="banks", bufs=2))
 
         w1_raw = keep.tile([P, PACK, F], BF16)
         w1_rows = W1.rearrange("(u q e) f -> u q e f", u=2, e=2)
@@ -66,24 +69,22 @@ def tile_encoderblock_pb_t_kernel(tc, h, W1, b1, W2, b2, gamma2, beta2, out):
         b1_rows = keep.tile([P, P], BF16)
         nc.vector.memset(b1_rows[:], 0.0)
         nc.scalar.dma_start(out=b1_rows[0:F_TILES, :], in_=b1.rearrange("(m p) -> m p", p=P))
-        b2_all = keep.tile([P, D], BF16)
-        nc.scalar.dma_start(out=b2_all[:], in_=b2.partition_broadcast(P))
-        gamma_all = keep.tile([P, D], BF16)
-        nc.scalar.dma_start(out=gamma_all[:], in_=gamma2.partition_broadcast(P))
-        beta_all = keep.tile([P, D], BF16)
-        nc.scalar.dma_start(out=beta_all[:], in_=beta2.partition_broadcast(P))
-
-        identity = keep.tile([P, P], F32)
-        make_identity(nc, identity[:])
+        vector_rows = keep.tile([P, 3, D], BF16)
+        nc.vector.memset(vector_rows[:], 0.0)
+        for j, vector in enumerate((b2, gamma2, beta2)):
+            nc.scalar.dma_start(out=vector_rows[0:1, j, :], in_=vector.unsqueeze(0))
+        ones = keep.tile([P, P], BF16)
+        nc.vector.memset(ones[:], 1.0)
         eps = keep.tile([P, 1], F32)
         nc.vector.memset(eps[:], EPS)
+        identity = keep.tile([P, P], F32)
+        make_identity(nc, identity[:])
 
-        b1_rows_f32 = keep.tile([P, P], F32)
-        nc.vector.tensor_copy(out=b1_rows_f32[:], in_=b1_rows[:])
-        b1_turned = psum.tile([P, 2, 2, P], F32, tag="turned")
-        nc.tensor.transpose(b1_turned[:, 0, 0, :], b1_rows_f32[:], identity[:])
         b1_cols = keep.tile([P, F_TILES], F32)
-        nc.vector.tensor_copy(out=b1_cols[:], in_=b1_turned[:, 0, 0, 0:F_TILES])
+        b2_all = keep.tile([P, D], F32)
+        norm_bank = fixed_banks.tile([P, 2, D], BF16)
+        gamma_all = norm_bank[:, 0, :]
+        beta_all = norm_bank[:, 1, :]
 
         w1_grouped = keep.tile([P, F, PACK], BF16, align_bytes=64)
         w1_codes = keep.tile([P, F], U32, align_bytes=64)
@@ -91,34 +92,46 @@ def tile_encoderblock_pb_t_kernel(tc, h, W1, b1, W2, b2, gamma2, beta2, out):
         w2_grouped = keep.tile([P, PASSES2, D, PACK], BF16, align_bytes=64)
         w2_codes = keep.tile([P, PASSES2, D], U32, align_bytes=64)
         w2_scales = keep.tile([P, PASSES2, D], U8, align_bytes=64)
-        for half, engine_copy in enumerate((nc.vector.tensor_copy, nc.scalar.copy)):
+
+        def regroup_w1_half(half):
             cols = slice(half * (F // 2), (half + 1) * (F // 2))
-            regroup(engine_copy, w1_grouped[:, cols, :], w1_raw[:, :, cols])
-        for half in range(2):
+            regroup(nc.vector.tensor_copy, w1_grouped[:, cols, :], w1_raw[:, :, cols])
+
+        def quantise_w1_half(half):
             cols = slice(half * (F // 2), (half + 1) * (F // 2))
             nc.vector.quantize_mx(
                 out=w1_codes[:, cols].bitcast(FP8X4),
                 scales=w1_scales[:, cols],
                 in_=w1_grouped[:, cols, :].rearrange("p f t -> p (f t)"),
             )
-        for g, engine_copy in enumerate((nc.vector.tensor_copy, nc.scalar.copy)):
-            regroup(engine_copy, w2_grouped[:, g], w2_raw[:, g])
-        for g in range(PASSES2):
-            nc.vector.quantize_mx(
-                out=w2_codes[:, g, :].bitcast(FP8X4),
-                scales=w2_scales[:, g, :],
-                in_=w2_grouped[:, g].rearrange("p n t -> p (n t)"),
-            )
 
+        def prepare_w2():
+            for g in range(PASSES2):
+                regroup(nc.vector.tensor_copy, w2_grouped[:, g], w2_raw[:, g])
+            for g in range(PASSES2):
+                nc.vector.quantize_mx(
+                    out=w2_codes[:, g, :].bitcast(FP8X4),
+                    scales=w2_scales[:, g, :],
+                    in_=w2_grouped[:, g].rearrange("p n t -> p (n t)"),
+                )
+
+
+        h_grouped_of = {}
         h_quantised = {}
-        f1_quantised = {}
         residuals = {}
+        f1_planes_of = {}
+        f1_grouped_of = {}
+        f1_quantised = {}
+        u_of = {}
+        sums_of = {}
+        scaled_of = {}
+        results_of = {}
 
-        def turn_and_quantise_h(c):
+        def turn_h(c):
             h_grouped = work.tile([P, CHUNK, PACK], BF16, align_bytes=64)
             grouped_words = h_grouped[:].rearrange("p w t -> p (w t)").bitcast(F32)
             for pair in range(SUB // 2):
-                turned = psum.tile([P, 2, 2, P], F32, tag="turned")
+                turned = banks.tile([P, 2, 2, P], F32, tag="turned")
                 for j in range(2):
                     words = h_all[:, c, 2 * pair + j, :].bitcast(F32)
                     for u in range(2):
@@ -131,6 +144,10 @@ def tile_encoderblock_pb_t_kernel(tc, h, W1, b1, W2, b2, gamma2, beta2, out):
                     ),
                     in_=turned[:].rearrange("p j u r -> p j r u"),
                 )
+            h_grouped_of[c] = h_grouped
+
+        def quantise_h(c):
+            h_grouped = h_grouped_of.pop(c)
             h_codes = work.tile([P, CHUNK], U32, align_bytes=64)
             h_scales = work.tile([P, CHUNK], U8, align_bytes=64)
             nc.vector.quantize_mx(
@@ -139,39 +156,50 @@ def tile_encoderblock_pb_t_kernel(tc, h, W1, b1, W2, b2, gamma2, beta2, out):
                 in_=h_grouped[:].rearrange("p w t -> p (w t)"),
             )
             h_quantised[c] = (h_codes, h_scales)
-            residual = work.tile([P, SUB, D], F32)
-            nc.vector.tensor_tensor(
-                out=residual[:],
-                in0=h_all[:, c],
-                in1=b2_all[:].unsqueeze(1).to_broadcast([P, SUB, D]),
-                op=ALU.add,
-            )
-            residuals[c] = residual
 
-        def first_matmul(c):
-            h_codes, h_scales = h_quantised.pop(c)
-            f1_planes = work.tile([P, F_TILES, CHUNK], BF16)
-            for m in range(F_TILES):
-                units = slice(m * P, (m + 1) * P)
-                acc1 = psum.tile([P, CHUNK], F32, bufs=3)
-                nc.tensor.matmul_mx(
-                    out=acc1[:],
-                    lhsT=w1_codes[:, units].bitcast(FP8X4),
-                    lhsT_scale=w1_scales[:, units],
-                    rhs=h_codes[:].bitcast(FP8X4),
-                    rhs_scale=h_scales[:],
-                    start=True,
-                    stop=True,
+        def add_b2_to_h(c):
+            residuals[c] = []
+            for i in range(SUB):
+                residual = work.tile([P, D], F32, bufs=2 * SUB)
+                nc.gpsimd.tensor_tensor(out=residual[:], in0=h_all[:, c, i, :], in1=b2_all[:], op=ALU.add)
+                residuals[c].append(residual)
+
+        def open_f1(c):
+            f1_planes_of[c] = work.tile([P, F_TILES, CHUNK], BF16, name="f1_planes")
+            f1_grouped_of[c] = work.tile(
+                [P, PASSES2, CHUNK, PACK], BF16, name="f1_grouped", align_bytes=64
+            )
+
+        def first_matmul(c, m):
+            h_codes, h_scales = h_quantised[c]
+            units = slice(m * P, (m + 1) * P)
+            acc1 = banks.tile([P, CHUNK], F32, bufs=3)
+            nc.tensor.matmul_mx(
+                out=acc1[:],
+                lhsT=w1_codes[:, units].bitcast(FP8X4),
+                lhsT_scale=w1_scales[:, units],
+                rhs=h_codes[:].bitcast(FP8X4),
+                rhs_scale=h_scales[:],
+                start=True,
+                stop=True,
+            )
+            nc.scalar.activation(
+                out=f1_planes_of[c][:, m, :], in_=acc1[:], func=ACT.Identity,
+                bias=b1_cols[:, m : m + 1], scale=1.0,
+            )
+
+        def regroup_f1(c, engine_copy, cols):
+            for g in range(PASSES2):
+                regroup(
+                    engine_copy,
+                    f1_grouped_of[c][:, g, cols, :],
+                    f1_planes_of[c][:, g * PACK : (g + 1) * PACK, cols],
                 )
-                nc.scalar.activation(
-                    out=f1_planes[:, m, :], in_=acc1[:], func=ACT.Identity,
-                    bias=b1_cols[:, m : m + 1], scale=1.0,
-                )
-            f1_grouped = work.tile([P, PASSES2, CHUNK, PACK], BF16, align_bytes=64)
+
+        def quantise_f1(c):
+            f1_grouped = f1_grouped_of.pop(c)
             f1_codes = work.tile([P, PASSES2, CHUNK], U32, align_bytes=64)
             f1_scales = work.tile([P, PASSES2, CHUNK], U8, align_bytes=64)
-            for g, engine_copy in enumerate((nc.vector.tensor_copy, nc.scalar.copy)):
-                regroup(engine_copy, f1_grouped[:, g], f1_planes[:, g * PACK : (g + 1) * PACK, :])
             for g in range(PASSES2):
                 nc.vector.quantize_mx(
                     out=f1_codes[:, g, :].bitcast(FP8X4),
@@ -180,61 +208,128 @@ def tile_encoderblock_pb_t_kernel(tc, h, W1, b1, W2, b2, gamma2, beta2, out):
                 )
             f1_quantised[c] = (f1_codes, f1_scales)
 
-        def second_matmul_and_norm(c):
-            f1_codes, f1_scales = f1_quantised.pop(c)
-            residual = residuals.pop(c)
-            u = work.tile([P, SUB, D], F32)
-            u_sum = work.tile([P, SUB], F32)
-            for i in range(SUB):
-                tokens = slice(i * P, (i + 1) * P)
-                acc2 = psum.tile([P, D], F32, bufs=3)
-                for g in range(PASSES2):
-                    nc.tensor.matmul_mx(
-                        out=acc2[:],
-                        lhsT=f1_codes[:, g, tokens].bitcast(FP8X4),
-                        lhsT_scale=f1_scales[:, g, tokens],
-                        rhs=w2_codes[:, g, :].bitcast(FP8X4),
-                        rhs_scale=w2_scales[:, g, :],
-                        start=(g == 0),
-                        stop=(g == PASSES2 - 1),
-                    )
-                nc.vector.scalar_tensor_tensor(
-                    out=u[:, i, :], in0=acc2[:], scalar=1.0, in1=residual[:, i, :],
-                    op0=ALU.mult, op1=ALU.add, accum_out=u_sum[:, i : i + 1],
+        def open_u(c):
+            u_of[c] = []
+            sums_of[c] = {"u_sum": work.tile([P, SUB], F32, name="u_sum")}
+
+        def second_matmul(c, i):
+            f1_codes, f1_scales = f1_quantised[c]
+            tokens = slice(i * P, (i + 1) * P)
+            acc2 = banks.tile([P, D], F32)
+            for g in range(PASSES2):
+                nc.tensor.matmul_mx(
+                    out=acc2[:],
+                    lhsT=f1_codes[:, g, tokens].bitcast(FP8X4),
+                    lhsT_scale=f1_scales[:, g, tokens],
+                    rhs=w2_codes[:, g, :].bitcast(FP8X4),
+                    rhs_scale=w2_scales[:, g, :],
+                    start=(g == 0),
+                    stop=(g == PASSES2 - 1),
                 )
+            u = work.tile([P, D], F32, bufs=2 * SUB)
+            nc.vector.scalar_tensor_tensor(
+                out=u[:], in0=acc2[:], scalar=1.0, in1=residuals[c][i][:],
+                op0=ALU.mult, op1=ALU.add, accum_out=sums_of[c]["u_sum"][:, i : i + 1],
+            )
+            u_of[c].append(u)
+
+        def minus_mean_of(c):
             minus_mean = work.tile([P, SUB], F32)
-            nc.vector.tensor_scalar_mul(out=minus_mean[:], in0=u_sum[:], scalar1=-1.0 / D)
-            squares = work.tile([P, SUB, D], BF16)
+            nc.scalar.mul(out=minus_mean[:], in_=sums_of[c]["u_sum"][:], mul=-1.0 / D)
+            sums_of[c]["minus_mean"] = minus_mean
+
+        def centre_and_scale(c):
+            minus_mean = sums_of[c]["minus_mean"]
+            scaled_of[c] = []
+            for i in range(SUB):
+                scaled = work.tile([P, D], F32, bufs=2 * SUB)
+                nc.vector.scalar_tensor_tensor(
+                    out=scaled[:], in0=u_of[c][i][:], scalar=minus_mean[:, i : i + 1], in1=gamma_all,
+                    op0=ALU.add, op1=ALU.mult,
+                )
+                scaled_of[c].append(scaled)
+
+        def deviation_of(c):
+            minus_mean = sums_of[c]["minus_mean"]
             square_sum = work.tile([P, SUB], F32)
             for i in range(SUB):
+                squares = work.tile([P, D], BF16, bufs=SUB)
                 nc.scalar.activation(
-                    out=squares[:, i, :], in_=u[:, i, :], func=ACT.Square,
+                    out=squares[:], in_=u_of[c][i][:], func=ACT.Square,
                     bias=minus_mean[:, i : i + 1], scale=1.0, accum_out=square_sum[:, i : i + 1],
                 )
             deviation = work.tile([P, SUB], F32)
             nc.scalar.activation(
                 out=deviation[:], in_=square_sum[:], func=ACT.Sqrt, bias=eps[:], scale=1.0 / D
             )
-            inv_deviation = work.tile([P, SUB], F32)
-            nc.vector.reciprocal(out=inv_deviation[:], in_=deviation[:])
-            result = work.tile([P, SUB, D], F32)
-            for i in range(SUB):
-                scaled = work.tile([P, D], F32, bufs=4)
-                nc.vector.scalar_tensor_tensor(
-                    out=scaled[:], in0=u[:, i, :], scalar=minus_mean[:, i : i + 1], in1=gamma_all[:],
-                    op0=ALU.add, op1=ALU.mult,
-                )
-                nc.vector.scalar_tensor_tensor(
-                    out=result[:, i, :], in0=scaled[:], scalar=inv_deviation[:, i : i + 1],
-                    in1=beta_all[:], op0=ALU.mult, op1=ALU.add,
-                )
-                if i % 2 == 1:
-                    nc.sync.dma_start(out=out_chunks[c][:, i - 1 : i + 1], in_=result[:, i - 1 : i + 1])
+            sums_of[c]["deviation"] = deviation
 
-        for step in range(N_CHUNKS + 2):
-            if step < N_CHUNKS:
-                turn_and_quantise_h(step)
-            if 1 <= step <= N_CHUNKS:
-                first_matmul(step - 1)
-            if step >= 2:
-                second_matmul_and_norm(step - 2)
+        def invert_deviation(c):
+            inv_deviation = work.tile([P, SUB], F32)
+            nc.vector.reciprocal(out=inv_deviation[:], in_=sums_of[c]["deviation"][:])
+            sums_of[c]["inv_deviation"] = inv_deviation
+
+        def finish(c, i):
+            if i % 2 == 0:
+                results_of[c] = work.tile([P, 2, D], F32, name="result", bufs=4)
+            nc.vector.scalar_tensor_tensor(
+                out=results_of[c][:, i % 2, :], in0=scaled_of[c][i][:],
+                scalar=sums_of[c]["inv_deviation"][:, i : i + 1],
+                in1=beta_all, op0=ALU.mult, op1=ALU.add,
+            )
+            if i % 2 == 1:
+                nc.sync.dma_start(out=out_chunks[c][:, i - 1 : i + 1], in_=results_of[c][:])
+
+        def live(c):
+            return 0 <= c < N_CHUNKS
+
+        regroup_w1_half(0)
+        turn_h(0)
+        quantise_w1_half(0)
+        b1_rows_f32 = keep.tile([P, P], F32)
+        nc.vector.tensor_copy(out=b1_rows_f32[:], in_=b1_rows[:])
+        b1_turned = banks.tile([P, D], F32, tag="acc1", bufs=3)
+        nc.tensor.transpose(b1_turned[:, 0:P], b1_rows_f32[:], identity[:])
+        b2_bank = banks.tile([P, D], F32, tag="acc1", bufs=3)
+        for j, spread in enumerate((b2_bank[:], gamma_all, beta_all)):
+            nc.tensor.matmul(out=spread, lhsT=ones[:], rhs=vector_rows[:, j, :], start=True, stop=True)
+        regroup_w1_half(1)
+        quantise_h(0)
+        nc.vector.tensor_copy(out=b1_cols[:], in_=b1_turned[:, 0:F_TILES])
+        quantise_w1_half(1)
+        nc.vector.tensor_copy(out=b2_all[:], in_=b2_bank[:])
+        add_b2_to_h(0)
+
+        for c in range(-1, N_CHUNKS + 1):
+            if live(c):
+                open_u(c)
+            if live(c + 1):
+                open_f1(c + 1)
+            for i in range(SUB):
+                if live(c):
+                    second_matmul(c, i)
+                if live(c + 1):
+                    first_matmul(c + 1, 2 * i)
+                if live(c) and i == SUB - 1:
+                    minus_mean_of(c)
+                if live(c - 1) and i == 0:
+                    invert_deviation(c - 1)
+                if live(c - 1):
+                    finish(c - 1, i)
+                if live(c + 1):
+                    first_matmul(c + 1, 2 * i + 1)
+            if live(c + 1):
+                regroup_f1(c + 1, nc.scalar.copy, slice(VECTOR_COLS, CHUNK))
+            if live(c + 2):
+                turn_h(c + 2)
+                add_b2_to_h(c + 2)
+            if live(c):
+                centre_and_scale(c)
+                deviation_of(c)
+            if c == -1:
+                prepare_w2()
+            if live(c + 1):
+                regroup_f1(c + 1, nc.vector.tensor_copy, slice(0, VECTOR_COLS))
+                quantise_f1(c + 1)
+            if live(c + 2):
+                quantise_h(c + 2)

@@ -22,7 +22,7 @@ N_CHUNKS = TOKENS // CHUNK
 F_TILES = F // P
 PASSES2 = F // (P * PACK)
 EPS = 1e-14
-VECTOR_COLS = 256
+VECTOR_COLS = 320
 
 FLOPS = 2 * TOKENS * D * F * 2
 
@@ -210,6 +210,7 @@ def tile_encoderblock_pb_t_kernel(tc, h, W1, b1, W2, b2, gamma2, beta2, out):
 
         def open_u(c):
             u_of[c] = []
+            scaled_of[c] = []
             sums_of[c] = {"u_sum": work.tile([P, SUB], F32, name="u_sum")}
 
         def second_matmul(c, i):
@@ -238,16 +239,13 @@ def tile_encoderblock_pb_t_kernel(tc, h, W1, b1, W2, b2, gamma2, beta2, out):
             nc.scalar.mul(out=minus_mean[:], in_=sums_of[c]["u_sum"][:], mul=-1.0 / D)
             sums_of[c]["minus_mean"] = minus_mean
 
-        def centre_and_scale(c):
-            minus_mean = sums_of[c]["minus_mean"]
-            scaled_of[c] = []
-            for i in range(SUB):
-                scaled = work.tile([P, D], F32, bufs=2 * SUB)
-                nc.vector.scalar_tensor_tensor(
-                    out=scaled[:], in0=u_of[c][i][:], scalar=minus_mean[:, i : i + 1], in1=gamma_all,
-                    op0=ALU.add, op1=ALU.mult,
-                )
-                scaled_of[c].append(scaled)
+        def centre_and_scale(c, i):
+            scaled = work.tile([P, D], F32, bufs=2 * SUB)
+            nc.vector.scalar_tensor_tensor(
+                out=scaled[:], in0=u_of[c][i][:], scalar=sums_of[c]["minus_mean"][:, i : i + 1],
+                in1=gamma_all, op0=ALU.add, op1=ALU.mult,
+            )
+            scaled_of[c].append(scaled)
 
         def deviation_of(c):
             minus_mean = sums_of[c]["minus_mean"]
@@ -301,6 +299,8 @@ def tile_encoderblock_pb_t_kernel(tc, h, W1, b1, W2, b2, gamma2, beta2, out):
         add_b2_to_h(0)
 
         for c in range(-1, N_CHUNKS + 1):
+            if live(c - 1):
+                centre_and_scale(c - 1, SUB - 1)
             if live(c):
                 open_u(c)
             if live(c + 1):
@@ -324,7 +324,8 @@ def tile_encoderblock_pb_t_kernel(tc, h, W1, b1, W2, b2, gamma2, beta2, out):
                 turn_h(c + 2)
                 add_b2_to_h(c + 2)
             if live(c):
-                centre_and_scale(c)
+                for i in range(SUB - 1):
+                    centre_and_scale(c, i)
                 deviation_of(c)
             if c == -1:
                 prepare_w2()

@@ -23,6 +23,7 @@ F_TILES = F // P
 PASSES2 = F // (P * PACK)
 EPS = 1e-14
 VECTOR_COLS = 320
+KEPT_BACK = 2
 
 FLOPS = 2 * TOKENS * D * F * 2
 
@@ -157,12 +158,10 @@ def tile_encoderblock_pb_t_kernel(tc, h, W1, b1, W2, b2, gamma2, beta2, out):
             )
             h_quantised[c] = (h_codes, h_scales)
 
-        def add_b2_to_h(c):
-            residuals[c] = []
-            for i in range(SUB):
-                residual = work.tile([P, D], F32, bufs=2 * SUB)
-                nc.gpsimd.tensor_tensor(out=residual[:], in0=h_all[:, c, i, :], in1=b2_all[:], op=ALU.add)
-                residuals[c].append(residual)
+        def add_b2_to_h(engine, c, i):
+            residual = work.tile([P, D], F32, bufs=2 * SUB)
+            engine.tensor_tensor(out=residual[:], in0=h_all[:, c, i, :], in1=b2_all[:], op=ALU.add)
+            residuals[c, i] = residual
 
         def open_f1(c):
             f1_planes_of[c] = work.tile([P, F_TILES, CHUNK], BF16, name="f1_planes")
@@ -229,7 +228,7 @@ def tile_encoderblock_pb_t_kernel(tc, h, W1, b1, W2, b2, gamma2, beta2, out):
                 )
             u = work.tile([P, D], F32, bufs=2 * SUB)
             nc.vector.scalar_tensor_tensor(
-                out=u[:], in0=acc2[:], scalar=1.0, in1=residuals[c][i][:],
+                out=u[:], in0=acc2[:], scalar=1.0, in1=residuals[c, i][:],
                 op0=ALU.mult, op1=ALU.add, accum_out=sums_of[c]["u_sum"][:, i : i + 1],
             )
             u_of[c].append(u)
@@ -296,11 +295,11 @@ def tile_encoderblock_pb_t_kernel(tc, h, W1, b1, W2, b2, gamma2, beta2, out):
         nc.vector.tensor_copy(out=b1_cols[:], in_=b1_turned[:, 0:F_TILES])
         quantise_w1_half(1)
         nc.vector.tensor_copy(out=b2_all[:], in_=b2_bank[:])
-        add_b2_to_h(0)
 
         for c in range(-1, N_CHUNKS + 1):
             if live(c - 1):
-                centre_and_scale(c - 1, SUB - 1)
+                for i in range(SUB - KEPT_BACK, SUB):
+                    centre_and_scale(c - 1, i)
             if live(c):
                 open_u(c)
             if live(c + 1):
@@ -316,19 +315,25 @@ def tile_encoderblock_pb_t_kernel(tc, h, W1, b1, W2, b2, gamma2, beta2, out):
                     invert_deviation(c - 1)
                 if live(c - 1):
                     finish(c - 1, i)
+                if c == 0:
+                    add_b2_to_h(nc.vector, 1, i)
                 if live(c + 1):
                     first_matmul(c + 1, 2 * i + 1)
             if live(c + 1):
                 regroup_f1(c + 1, nc.scalar.copy, slice(VECTOR_COLS, CHUNK))
             if live(c + 2):
                 turn_h(c + 2)
-                add_b2_to_h(c + 2)
+            if live(c) and live(c + 2):
+                for i in range(SUB):
+                    add_b2_to_h(nc.gpsimd, c + 2, i)
             if live(c):
-                for i in range(SUB - 1):
+                for i in range(SUB - KEPT_BACK):
                     centre_and_scale(c, i)
                 deviation_of(c)
             if c == -1:
                 prepare_w2()
+                for i in range(SUB):
+                    add_b2_to_h(nc.vector, 0, i)
             if live(c + 1):
                 regroup_f1(c + 1, nc.vector.tensor_copy, slice(0, VECTOR_COLS))
                 quantise_f1(c + 1)

@@ -56,8 +56,8 @@ def tile_encoderblock_pb_t_kernel(tc, h, W1, b1, W2, b2, gamma2, beta2, out):
             for u in range(2):
                 nc.sync.dma_start(out=w1_raw[:, 2 * u : 2 * u + 2, cols], in_=w1_rows[u][:, :, cols])
 
-        load_w1_half(0)
         nc.sync.dma_start(out=h_all[:, 0], in_=h_chunks[0])
+        load_w1_half(0)
         load_w1_half(1)
         w2_raw = keep.tile([P, PASSES2, PACK, D], BF16)
         nc.sync.dma_start(
@@ -68,16 +68,16 @@ def tile_encoderblock_pb_t_kernel(tc, h, W1, b1, W2, b2, gamma2, beta2, out):
             nc.sync.dma_start(out=h_all[:, c], in_=h_chunks[c])
 
         b1_rows = keep.tile([P, P], BF16)
-        nc.vector.memset(b1_rows[:], 0.0)
+        nc.gpsimd.memset(b1_rows[:], 0.0)
         nc.scalar.dma_start(out=b1_rows[0:F_TILES, :], in_=b1.rearrange("(m p) -> m p", p=P))
         vector_rows = keep.tile([P, 3, D], BF16)
-        nc.vector.memset(vector_rows[:], 0.0)
+        nc.gpsimd.memset(vector_rows[:], 0.0)
         for j, vector in enumerate((b2, gamma2, beta2)):
             nc.scalar.dma_start(out=vector_rows[0:1, j, :], in_=vector.unsqueeze(0))
         ones = keep.tile([P, P], BF16)
-        nc.vector.memset(ones[:], 1.0)
+        nc.gpsimd.memset(ones[:], 1.0)
         eps = keep.tile([P, 1], F32)
-        nc.vector.memset(eps[:], EPS)
+        nc.gpsimd.memset(eps[:], EPS)
         identity = keep.tile([P, P], F32)
         make_identity(nc, identity[:])
 
@@ -159,7 +159,7 @@ def tile_encoderblock_pb_t_kernel(tc, h, W1, b1, W2, b2, gamma2, beta2, out):
             h_quantised[c] = (h_codes, h_scales)
 
         def add_b2_to_h(engine, c, i):
-            residual = work.tile([P, D], F32, bufs=2 * SUB)
+            residual = work.tile([P, D], F32, bufs=SUB)
             engine.tensor_tensor(out=residual[:], in0=h_all[:, c, i, :], in1=b2_all[:], op=ALU.add)
             residuals[c, i] = residual
 
@@ -280,21 +280,21 @@ def tile_encoderblock_pb_t_kernel(tc, h, W1, b1, W2, b2, gamma2, beta2, out):
         def live(c):
             return 0 <= c < N_CHUNKS
 
-        regroup_w1_half(0)
         turn_h(0)
+        regroup_w1_half(0)
+        quantise_h(0)
         quantise_w1_half(0)
         b1_rows_f32 = keep.tile([P, P], F32)
-        nc.vector.tensor_copy(out=b1_rows_f32[:], in_=b1_rows[:])
+        nc.scalar.copy(out=b1_rows_f32[:], in_=b1_rows[:])
         b1_turned = banks.tile([P, D], F32, tag="acc1", bufs=3)
         nc.tensor.transpose(b1_turned[:, 0:P], b1_rows_f32[:], identity[:])
         b2_bank = banks.tile([P, D], F32, tag="acc1", bufs=3)
         for j, spread in enumerate((b2_bank[:], gamma_all, beta_all)):
             nc.tensor.matmul(out=spread, lhsT=ones[:], rhs=vector_rows[:, j, :], start=True, stop=True)
         regroup_w1_half(1)
-        quantise_h(0)
-        nc.vector.tensor_copy(out=b1_cols[:], in_=b1_turned[:, 0:F_TILES])
+        nc.scalar.copy(out=b1_cols[:], in_=b1_turned[:, 0:F_TILES])
+        nc.scalar.copy(out=b2_all[:], in_=b2_bank[:])
         quantise_w1_half(1)
-        nc.vector.tensor_copy(out=b2_all[:], in_=b2_bank[:])
 
         for c in range(-1, N_CHUNKS + 1):
             if live(c - 1):
@@ -315,17 +315,15 @@ def tile_encoderblock_pb_t_kernel(tc, h, W1, b1, W2, b2, gamma2, beta2, out):
                     invert_deviation(c - 1)
                 if live(c - 1):
                     finish(c - 1, i)
-                if c == 0:
-                    add_b2_to_h(nc.vector, 1, i)
                 if live(c + 1):
                     first_matmul(c + 1, 2 * i + 1)
             if live(c + 1):
                 regroup_f1(c + 1, nc.scalar.copy, slice(VECTOR_COLS, CHUNK))
             if live(c + 2):
                 turn_h(c + 2)
-            if live(c) and live(c + 2):
+            if live(c) and live(c + 1):
                 for i in range(SUB):
-                    add_b2_to_h(nc.gpsimd, c + 2, i)
+                    add_b2_to_h(nc.gpsimd, c + 1, i)
             if live(c):
                 for i in range(SUB - KEPT_BACK):
                     centre_and_scale(c, i)

@@ -228,7 +228,7 @@ def tile_encoderblock_pb_t_kernel(tc, h, W1, b1, W2, b2, gamma2, beta2, out):
                 )
             u = work.tile([P, D], F32, bufs=2 * SUB)
             nc.vector.scalar_tensor_tensor(
-                out=u[:], in0=acc2[:], scalar=1.0, in1=residuals[c, i][:],
+                out=u[:], in0=residuals[c, i][:], scalar=1.0, in1=acc2[:],
                 op0=ALU.mult, op1=ALU.add, accum_out=sums_of[c]["u_sum"][:, i : i + 1],
             )
             u_of[c].append(u)
@@ -246,7 +246,7 @@ def tile_encoderblock_pb_t_kernel(tc, h, W1, b1, W2, b2, gamma2, beta2, out):
             )
             scaled_of[c].append(scaled)
 
-        def deviation_of(c):
+        def inv_deviation_of(c):
             minus_mean = sums_of[c]["minus_mean"]
             square_sum = work.tile([P, SUB], F32)
             for i in range(SUB):
@@ -255,15 +255,11 @@ def tile_encoderblock_pb_t_kernel(tc, h, W1, b1, W2, b2, gamma2, beta2, out):
                     out=squares[:], in_=u_of[c][i][:], func=ACT.Square,
                     bias=minus_mean[:, i : i + 1], scale=1.0, accum_out=square_sum[:, i : i + 1],
                 )
-            deviation = work.tile([P, SUB], F32)
-            nc.scalar.activation(
-                out=deviation[:], in_=square_sum[:], func=ACT.Sqrt, bias=eps[:], scale=1.0 / D
-            )
-            sums_of[c]["deviation"] = deviation
-
-        def invert_deviation(c):
             inv_deviation = work.tile([P, SUB], F32)
-            nc.vector.reciprocal(out=inv_deviation[:], in_=sums_of[c]["deviation"][:])
+            nc.scalar.activation(
+                out=inv_deviation[:], in_=square_sum[:], func=ACT.Abs_reciprocal_sqrt,
+                bias=eps[:], scale=1.0 / D,
+            )
             sums_of[c]["inv_deviation"] = inv_deviation
 
         def finish(c, i):
@@ -311,8 +307,6 @@ def tile_encoderblock_pb_t_kernel(tc, h, W1, b1, W2, b2, gamma2, beta2, out):
                     first_matmul(c + 1, 2 * i)
                 if live(c) and i == SUB - 1:
                     minus_mean_of(c)
-                if live(c - 1) and i == 0:
-                    invert_deviation(c - 1)
                 if live(c - 1):
                     finish(c - 1, i)
                 if live(c + 1):
@@ -327,7 +321,7 @@ def tile_encoderblock_pb_t_kernel(tc, h, W1, b1, W2, b2, gamma2, beta2, out):
             if live(c):
                 for i in range(SUB - KEPT_BACK):
                     centre_and_scale(c, i)
-                deviation_of(c)
+                inv_deviation_of(c)
             if c == -1:
                 prepare_w2()
                 for i in range(SUB):

@@ -22,7 +22,7 @@ N_CHUNKS = TOKENS // CHUNK
 F_TILES = F // P
 PASSES2 = F // (P * PACK)
 EPS = 1e-14
-VECTOR_COLS = 320
+VECTOR_COLS = 448
 KEPT_BACK = 2
 
 FLOPS = 2 * TOKENS * D * F * 2
@@ -68,18 +68,20 @@ def tile_encoderblock_pb_t_kernel(tc, h, W1, b1, W2, b2, gamma2, beta2, out):
             nc.sync.dma_start(out=h_all[:, c], in_=h_chunks[c])
 
         b1_rows = keep.tile([P, P], BF16)
-        nc.gpsimd.memset(b1_rows[:], 0.0)
+        nc.vector.memset(b1_rows[:].bitcast(U32), 0)
         nc.scalar.dma_start(out=b1_rows[0:F_TILES, :], in_=b1.rearrange("(m p) -> m p", p=P))
         vector_rows = keep.tile([P, 3, D], BF16)
-        nc.gpsimd.memset(vector_rows[:], 0.0)
+        nc.vector.memset(vector_rows[:].rearrange("p j n -> p (j n)").bitcast(U32), 0)
         for j, vector in enumerate((b2, gamma2, beta2)):
             nc.scalar.dma_start(out=vector_rows[0:1, j, :], in_=vector.unsqueeze(0))
         ones = keep.tile([P, P], BF16)
-        nc.gpsimd.memset(ones[:], 1.0)
+        nc.vector.memset(ones[:], 1.0)
         eps = keep.tile([P, 1], F32)
-        nc.gpsimd.memset(eps[:], EPS)
+        nc.vector.memset(eps[:], EPS)
         identity = keep.tile([P, P], F32)
         make_identity(nc, identity[:])
+        identity_bf16 = keep.tile([P, P], BF16)
+        make_identity(nc, identity_bf16[:])
 
         b1_cols = keep.tile([P, F_TILES], F32)
         b2_all = keep.tile([P, D], F32)
@@ -126,13 +128,14 @@ def tile_encoderblock_pb_t_kernel(tc, h, W1, b1, W2, b2, gamma2, beta2, out):
         u_of = {}
         sums_of = {}
         scaled_of = {}
+        acc1_of = {}
         results_of = {}
 
         def turn_h(c):
             h_grouped = work.tile([P, CHUNK, PACK], BF16, align_bytes=64)
             grouped_words = h_grouped[:].rearrange("p w t -> p (w t)").bitcast(F32)
             for pair in range(SUB // 2):
-                turned = banks.tile([P, 2, 2, P], F32, tag="turned")
+                turned = banks.tile([P, 2, 2, P], F32, tag="bank", bufs=7)
                 for j in range(2):
                     words = h_all[:, c, 2 * pair + j, :].bitcast(F32)
                     for u in range(2):
@@ -159,8 +162,20 @@ def tile_encoderblock_pb_t_kernel(tc, h, W1, b1, W2, b2, gamma2, beta2, out):
             h_quantised[c] = (h_codes, h_scales)
 
         def add_b2_to_h(engine, c, i):
-            residual = work.tile([P, D], F32, bufs=SUB)
+            residual = work.tile([P, D], F32, tag="residual", bufs=SUB)
             engine.tensor_tensor(out=residual[:], in0=h_all[:, c, i, :], in1=b2_all[:], op=ALU.add)
+            residuals[c, i] = residual
+
+        def spread_residual(c, i):
+            sum_bank = banks.tile([P, D], F32, tag="bank", bufs=7)
+            nc.tensor.matmul(
+                out=sum_bank[:], lhsT=identity_bf16[:], rhs=h_all[:, c, i, :], start=True, stop=False
+            )
+            nc.tensor.matmul(
+                out=sum_bank[:], lhsT=ones[:], rhs=vector_rows[:, 0, :], start=False, stop=True
+            )
+            residual = work.tile([P, D], F32, tag="residual", bufs=SUB)
+            nc.scalar.copy(out=residual[:], in_=sum_bank[:])
             residuals[c, i] = residual
 
         def open_f1(c):
@@ -172,7 +187,7 @@ def tile_encoderblock_pb_t_kernel(tc, h, W1, b1, W2, b2, gamma2, beta2, out):
         def first_matmul(c, m):
             h_codes, h_scales = h_quantised[c]
             units = slice(m * P, (m + 1) * P)
-            acc1 = banks.tile([P, CHUNK], F32, bufs=3)
+            acc1 = banks.tile([P, CHUNK], F32, tag="bank", bufs=7)
             nc.tensor.matmul_mx(
                 out=acc1[:],
                 lhsT=w1_codes[:, units].bitcast(FP8X4),
@@ -182,40 +197,51 @@ def tile_encoderblock_pb_t_kernel(tc, h, W1, b1, W2, b2, gamma2, beta2, out):
                 start=True,
                 stop=True,
             )
-            nc.scalar.activation(
-                out=f1_planes_of[c][:, m, :], in_=acc1[:], func=ACT.Identity,
-                bias=b1_cols[:, m : m + 1], scale=1.0,
-            )
+            acc1_of[c, m] = acc1
 
-        def regroup_f1(c, engine_copy, cols):
-            for g in range(PASSES2):
+        def add_b1(c, m, by_vector=False):
+            bank = acc1_of.pop((c, m))
+            bias = b1_cols[:, m : m + 1]
+            if by_vector:
+                nc.vector.tensor_scalar(
+                    out=f1_planes_of[c][:, m, :], in0=bank[:], scalar1=bias, scalar2=None, op0=ALU.add
+                )
+            else:
+                nc.scalar.activation(
+                    out=f1_planes_of[c][:, m, :], in_=bank[:], func=ACT.Identity, bias=bias, scale=1.0
+                )
+
+        def regroup_f1(c, engine_copy, cols, passes=range(PASSES2)):
+            for g in passes:
                 regroup(
                     engine_copy,
                     f1_grouped_of[c][:, g, cols, :],
                     f1_planes_of[c][:, g * PACK : (g + 1) * PACK, cols],
                 )
 
-        def quantise_f1(c):
-            f1_grouped = f1_grouped_of.pop(c)
-            f1_codes = work.tile([P, PASSES2, CHUNK], U32, align_bytes=64)
-            f1_scales = work.tile([P, PASSES2, CHUNK], U8, align_bytes=64)
-            for g in range(PASSES2):
+        def quantise_f1(c, passes=range(PASSES2)):
+            f1_grouped = f1_grouped_of[c]
+            if c not in f1_quantised:
+                f1_codes = work.tile([P, PASSES2, CHUNK], U32, align_bytes=64)
+                f1_scales = work.tile([P, PASSES2, CHUNK], U8, align_bytes=64)
+                f1_quantised[c] = (f1_codes, f1_scales)
+            f1_codes, f1_scales = f1_quantised[c]
+            for g in passes:
                 nc.vector.quantize_mx(
                     out=f1_codes[:, g, :].bitcast(FP8X4),
                     scales=f1_scales[:, g, :],
                     in_=f1_grouped[:, g].rearrange("p w t -> p (w t)"),
                 )
-            f1_quantised[c] = (f1_codes, f1_scales)
 
         def open_u(c):
             u_of[c] = []
-            scaled_of[c] = []
+            scaled_of[c] = {}
             sums_of[c] = {"u_sum": work.tile([P, SUB], F32, name="u_sum")}
 
         def second_matmul(c, i):
             f1_codes, f1_scales = f1_quantised[c]
             tokens = slice(i * P, (i + 1) * P)
-            acc2 = banks.tile([P, D], F32)
+            acc2 = banks.tile([P, D], F32, tag="bank", bufs=7)
             for g in range(PASSES2):
                 nc.tensor.matmul_mx(
                     out=acc2[:],
@@ -226,7 +252,7 @@ def tile_encoderblock_pb_t_kernel(tc, h, W1, b1, W2, b2, gamma2, beta2, out):
                     start=(g == 0),
                     stop=(g == PASSES2 - 1),
                 )
-            u = work.tile([P, D], F32, bufs=2 * SUB)
+            u = work.tile([P, D], F32, tag="u", bufs=2 * SUB)
             nc.vector.scalar_tensor_tensor(
                 out=u[:], in0=residuals[c, i][:], scalar=1.0, in1=acc2[:],
                 op0=ALU.mult, op1=ALU.add, accum_out=sums_of[c]["u_sum"][:, i : i + 1],
@@ -240,11 +266,19 @@ def tile_encoderblock_pb_t_kernel(tc, h, W1, b1, W2, b2, gamma2, beta2, out):
 
         def centre_and_scale(c, i):
             scaled = work.tile([P, D], F32, bufs=2 * SUB)
+            scaled_of[c][i] = scaled
+            if i in lent_tiles(c):
+                centred = work.tile([P, D], F32, bufs=SUB)
+                nc.scalar.activation(
+                    out=centred[:], in_=u_of[c][i][:], func=ACT.Identity,
+                    bias=sums_of[c]["minus_mean"][:, i : i + 1], scale=1.0,
+                )
+                nc.gpsimd.tensor_tensor(out=scaled[:], in0=centred[:], in1=gamma_sb[:], op=ALU.mult)
+                return
             nc.vector.scalar_tensor_tensor(
                 out=scaled[:], in0=u_of[c][i][:], scalar=sums_of[c]["minus_mean"][:, i : i + 1],
                 in1=gamma_all, op0=ALU.add, op1=ALU.mult,
             )
-            scaled_of[c].append(scaled)
 
         def inv_deviation_of(c):
             minus_mean = sums_of[c]["minus_mean"]
@@ -270,62 +304,95 @@ def tile_encoderblock_pb_t_kernel(tc, h, W1, b1, W2, b2, gamma2, beta2, out):
                 scalar=sums_of[c]["inv_deviation"][:, i : i + 1],
                 in1=beta_all, op0=ALU.mult, op1=ALU.add,
             )
-            if i % 2 == 1:
+            if c == N_CHUNKS - 1:
+                nc.sync.dma_start(out=out_chunks[c][:, i], in_=results_of[c][:, i % 2, :])
+            elif i % 2 == 1:
                 nc.sync.dma_start(out=out_chunks[c][:, i - 1 : i + 1], in_=results_of[c][:])
+
+        def lent_tiles(c):
+            return (2, 3) if c == N_CHUNKS - 2 else (3,) if c == N_CHUNKS - 1 else (3,)
 
         def live(c):
             return 0 <= c < N_CHUNKS
 
+        b1_rows_f32 = keep.tile([P, P], F32)
+        b1_turned = banks.tile([P, D], F32, tag="bank", bufs=7)
+        b2_bank = banks.tile([P, D], F32, tag="bank", bufs=7)
         turn_h(0)
         regroup_w1_half(0)
         quantise_h(0)
         quantise_w1_half(0)
-        b1_rows_f32 = keep.tile([P, P], F32)
         nc.scalar.copy(out=b1_rows_f32[:], in_=b1_rows[:])
-        b1_turned = banks.tile([P, D], F32, tag="acc1", bufs=3)
         nc.tensor.transpose(b1_turned[:, 0:P], b1_rows_f32[:], identity[:])
-        b2_bank = banks.tile([P, D], F32, tag="acc1", bufs=3)
-        for j, spread in enumerate((b2_bank[:], gamma_all, beta_all)):
-            nc.tensor.matmul(out=spread, lhsT=ones[:], rhs=vector_rows[:, j, :], start=True, stop=True)
-        regroup_w1_half(1)
+        nc.tensor.matmul(out=b2_bank[:], lhsT=ones[:], rhs=vector_rows[:, 0, :], start=True, stop=True)
         nc.scalar.copy(out=b1_cols[:], in_=b1_turned[:, 0:F_TILES])
         nc.scalar.copy(out=b2_all[:], in_=b2_bank[:])
+        regroup_w1_half(1)
         quantise_w1_half(1)
+        open_f1(0)
+        for m in range(F_TILES):
+            if m == 4:
+                turn_h(1)
+            first_matmul(0, m)
+            if m not in (7,):
+                add_b1(0, m)
+        for j, spread in enumerate((gamma_all, beta_all)):
+            nc.tensor.matmul(out=spread, lhsT=ones[:], rhs=vector_rows[:, 1 + j, :], start=True, stop=True)
+        gamma_sb = keep.tile([P, D], BF16)
+        for i in range(SUB):
+            spread_residual(0, i)
+        nc.scalar.copy(out=gamma_sb[:], in_=gamma_all)
+        prepare_w2()
+        regroup_f1(0, nc.vector.tensor_copy, slice(0, CHUNK), (0,))
+        quantise_f1(0, (0,))
+        quantise_h(1)
+        open_f1(1)
+        for m in range(2):
+            first_matmul(1, m)
+            add_b1(1, m)
+        add_b1(0, 7, by_vector=True)
+        regroup_f1(0, nc.vector.tensor_copy, slice(0, CHUNK), (1,))
+        quantise_f1(0, (1,))
 
-        for c in range(-1, N_CHUNKS + 1):
-            if live(c - 1):
-                for i in range(SUB - KEPT_BACK, SUB):
+        for c in range(N_CHUNKS + 1):
+            if 0 < c < N_CHUNKS:
+                for i in range(SUB):
                     centre_and_scale(c - 1, i)
             if live(c):
                 open_u(c)
-            if live(c + 1):
+            if c > 0 and live(c + 1):
                 open_f1(c + 1)
+            tiles = list(range(2 if c == 0 else 0, F_TILES)) if live(c + 1) else []
             for i in range(SUB):
+                mine = tiles[len(tiles) * i // SUB : len(tiles) * (i + 1) // SUB]
                 if live(c):
                     second_matmul(c, i)
-                if live(c + 1):
-                    first_matmul(c + 1, 2 * i)
-                if live(c) and i == SUB - 1:
-                    minus_mean_of(c)
-                if live(c - 1):
+                for m in mine[:1]:
+                    first_matmul(c + 1, m)
+                    add_b1(c + 1, m)
+                if live(c - 1) and c != N_CHUNKS - 1:
                     finish(c - 1, i)
-                if live(c + 1):
-                    first_matmul(c + 1, 2 * i + 1)
-            if live(c + 1):
-                regroup_f1(c + 1, nc.scalar.copy, slice(VECTOR_COLS, CHUNK))
-            if live(c + 2):
-                turn_h(c + 2)
+                for m in mine[1:]:
+                    first_matmul(c + 1, m)
+                    add_b1(c + 1, m)
+            if c == N_CHUNKS - 1:
+                minus_mean_of(c)
+                for i in range(SUB):
+                    finish(c - 1, i)
             if live(c) and live(c + 1):
                 for i in range(SUB):
                     add_b2_to_h(nc.gpsimd, c + 1, i)
-            if live(c):
-                for i in range(SUB - KEPT_BACK):
+            if live(c + 1):
+                regroup_f1(c + 1, nc.scalar.copy, slice(VECTOR_COLS, CHUNK))
+            if live(c) and c != N_CHUNKS - 1:
+                minus_mean_of(c)
+            if live(c + 2):
+                turn_h(c + 2)
+            if c == N_CHUNKS - 1:
+                for i in reversed(range(SUB)):
                     centre_and_scale(c, i)
+            if live(c):
                 inv_deviation_of(c)
-            if c == -1:
-                prepare_w2()
-                for i in range(SUB):
-                    add_b2_to_h(nc.vector, 0, i)
             if live(c + 1):
                 regroup_f1(c + 1, nc.vector.tensor_copy, slice(0, VECTOR_COLS))
                 quantise_f1(c + 1)

@@ -22,7 +22,7 @@ N_CHUNKS = TOKENS // CHUNK
 F_TILES = F // P
 PASSES2 = F // (P * PACK)
 EPS = 1e-14
-VECTOR_COLS = 448
+VECTOR_COLS = 320
 KEPT_BACK = 2
 
 FLOPS = 2 * TOKENS * D * F * 2
@@ -162,7 +162,7 @@ def tile_encoderblock_pb_t_kernel(tc, h, W1, b1, W2, b2, gamma2, beta2, out):
             h_quantised[c] = (h_codes, h_scales)
 
         def add_b2_to_h(engine, c, i):
-            residual = work.tile([P, D], F32, tag="residual", bufs=SUB)
+            residual = work.tile([P, D], F32, tag="row%d" % i, bufs=3)
             engine.tensor_tensor(out=residual[:], in0=h_all[:, c, i, :], in1=b2_all[:], op=ALU.add)
             residuals[c, i] = residual
 
@@ -174,7 +174,7 @@ def tile_encoderblock_pb_t_kernel(tc, h, W1, b1, W2, b2, gamma2, beta2, out):
             nc.tensor.matmul(
                 out=sum_bank[:], lhsT=ones[:], rhs=vector_rows[:, 0, :], start=False, stop=True
             )
-            residual = work.tile([P, D], F32, tag="residual", bufs=SUB)
+            residual = work.tile([P, D], F32, tag="row%d" % i, bufs=3)
             nc.scalar.copy(out=residual[:], in_=sum_bank[:])
             residuals[c, i] = residual
 
@@ -252,7 +252,7 @@ def tile_encoderblock_pb_t_kernel(tc, h, W1, b1, W2, b2, gamma2, beta2, out):
                     start=(g == 0),
                     stop=(g == PASSES2 - 1),
                 )
-            u = work.tile([P, D], F32, tag="u", bufs=2 * SUB)
+            u = work.tile([P, D], F32, tag="row%d" % i, bufs=3)
             nc.vector.scalar_tensor_tensor(
                 out=u[:], in0=residuals[c, i][:], scalar=1.0, in1=acc2[:],
                 op0=ALU.mult, op1=ALU.add, accum_out=sums_of[c]["u_sum"][:, i : i + 1],
@@ -310,7 +310,7 @@ def tile_encoderblock_pb_t_kernel(tc, h, W1, b1, W2, b2, gamma2, beta2, out):
                 nc.sync.dma_start(out=out_chunks[c][:, i - 1 : i + 1], in_=results_of[c][:])
 
         def lent_tiles(c):
-            return (2, 3) if c == N_CHUNKS - 2 else (3,) if c == N_CHUNKS - 1 else (3,)
+            return (2, 3) if c == N_CHUNKS - 2 else (3,) if c == N_CHUNKS - 1 else ()
 
         def live(c):
             return 0 <= c < N_CHUNKS
@@ -372,6 +372,8 @@ def tile_encoderblock_pb_t_kernel(tc, h, W1, b1, W2, b2, gamma2, beta2, out):
                     add_b1(c + 1, m)
                 if live(c - 1) and c != N_CHUNKS - 1:
                     finish(c - 1, i)
+                if c == 0:
+                    add_b2_to_h(nc.vector, 1, i)
                 for m in mine[1:]:
                     first_matmul(c + 1, m)
                     add_b1(c + 1, m)
@@ -379,7 +381,7 @@ def tile_encoderblock_pb_t_kernel(tc, h, W1, b1, W2, b2, gamma2, beta2, out):
                 minus_mean_of(c)
                 for i in range(SUB):
                     finish(c - 1, i)
-            if live(c) and live(c + 1):
+            if c > 0 and live(c + 1):
                 for i in range(SUB):
                     add_b2_to_h(nc.gpsimd, c + 1, i)
             if live(c + 1):

@@ -22,7 +22,7 @@ N_CHUNKS = TOKENS // CHUNK
 F_TILES = F // P
 PASSES2 = F // (P * PACK)
 EPS = 1e-14
-VECTOR_COLS = 320
+VECTOR_COLS = 448
 KEPT_BACK = 2
 
 FLOPS = 2 * TOKENS * D * F * 2
@@ -56,7 +56,9 @@ def tile_encoderblock_pb_t_kernel(tc, h, W1, b1, W2, b2, gamma2, beta2, out):
             for u in range(2):
                 nc.sync.dma_start(out=w1_raw[:, 2 * u : 2 * u + 2, cols], in_=w1_rows[u][:, :, cols])
 
-        nc.sync.dma_start(out=h_all[:, 0], in_=h_chunks[0])
+        for half in range(2):
+            pair = slice(2 * half, 2 * half + 2)
+            nc.sync.dma_start(out=h_all[:, 0, pair], in_=h_chunks[0][:, pair])
         load_w1_half(0)
         load_w1_half(1)
         w2_raw = keep.tile([P, PASSES2, PACK, D], BF16)
@@ -129,6 +131,9 @@ def tile_encoderblock_pb_t_kernel(tc, h, W1, b1, W2, b2, gamma2, beta2, out):
         sums_of = {}
         scaled_of = {}
         acc1_of = {}
+        finish_bank_of = {}
+        done_of = {}
+        diagonal_of = {}
         results_of = {}
 
         def turn_h(c):
@@ -296,18 +301,54 @@ def tile_encoderblock_pb_t_kernel(tc, h, W1, b1, W2, b2, gamma2, beta2, out):
             )
             sums_of[c]["inv_deviation"] = inv_deviation
 
+        def open_result(c, i):
+            if (c, i // 2) not in results_of:
+                results_of[c, i // 2] = work.tile([P, 2, D], F32, name="result", bufs=4)
+
+        def store(c, i):
+            if c == N_CHUNKS - 1:
+                nc.sync.dma_start(out=out_chunks[c][:, i], in_=results_of[c, i // 2][:, i % 2, :])
+            else:
+                done_of.setdefault((c, i // 2), []).append(i)
+                if len(done_of[c, i // 2]) == 2:
+                    j = i // 2 * 2
+                    nc.sync.dma_start(out=out_chunks[c][:, j : j + 2], in_=results_of[c, i // 2][:])
+
+        def make_diagonal(c, i):
+            diagonal = work.tile([P, P], F32, bufs=4)
+            nc.scalar.activation(
+                out=diagonal[:], in_=identity[:], func=ACT.Copy,
+                scale=sums_of[c]["inv_deviation"][:, i : i + 1],
+            )
+            diagonal_of[c, i] = diagonal
+
+        def spread_finish(c, i):
+            diagonal = diagonal_of.pop((c, i))
+            finish_bank = banks.tile([P, D], F32, tag="bank", bufs=7)
+            nc.tensor.matmul(
+                out=finish_bank[:], lhsT=diagonal[:], rhs=scaled_of[c][i][:], start=True, stop=False
+            )
+            nc.tensor.matmul(
+                out=finish_bank[:], lhsT=ones[:], rhs=vector_rows[:, 2, :], start=False, stop=True
+            )
+            finish_bank_of[c] = finish_bank
+
+        def finish_by_scalar(c, i):
+            open_result(c, i)
+            nc.scalar.copy(out=results_of[c, i // 2][:, i % 2, :], in_=finish_bank_of.pop(c)[:])
+            store(c, i)
+
+        def by_tensor(c, i):
+            return i in (0,) and 0 <= c <= 5
+
         def finish(c, i):
-            if i % 2 == 0:
-                results_of[c] = work.tile([P, 2, D], F32, name="result", bufs=4)
+            open_result(c, i)
             nc.vector.scalar_tensor_tensor(
-                out=results_of[c][:, i % 2, :], in0=scaled_of[c][i][:],
+                out=results_of[c, i // 2][:, i % 2, :], in0=scaled_of[c][i][:],
                 scalar=sums_of[c]["inv_deviation"][:, i : i + 1],
                 in1=beta_all, op0=ALU.mult, op1=ALU.add,
             )
-            if c == N_CHUNKS - 1:
-                nc.sync.dma_start(out=out_chunks[c][:, i], in_=results_of[c][:, i % 2, :])
-            elif i % 2 == 1:
-                nc.sync.dma_start(out=out_chunks[c][:, i - 1 : i + 1], in_=results_of[c][:])
+            store(c, i)
 
         def lent_tiles(c):
             return (2, 3) if c == N_CHUNKS - 2 else (3,) if c == N_CHUNKS - 1 else ()
@@ -370,7 +411,7 @@ def tile_encoderblock_pb_t_kernel(tc, h, W1, b1, W2, b2, gamma2, beta2, out):
                 for m in mine[:1]:
                     first_matmul(c + 1, m)
                     add_b1(c + 1, m)
-                if live(c - 1) and c != N_CHUNKS - 1:
+                if live(c - 1) and c != N_CHUNKS - 1 and not by_tensor(c - 1, i):
                     finish(c - 1, i)
                 if c == 0:
                     add_b2_to_h(nc.vector, 1, i)
@@ -380,7 +421,8 @@ def tile_encoderblock_pb_t_kernel(tc, h, W1, b1, W2, b2, gamma2, beta2, out):
             if c == N_CHUNKS - 1:
                 minus_mean_of(c)
                 for i in range(SUB):
-                    finish(c - 1, i)
+                    if not by_tensor(c - 1, i):
+                        finish(c - 1, i)
             if c > 0 and live(c + 1):
                 for i in range(SUB):
                     add_b2_to_h(nc.gpsimd, c + 1, i)
@@ -390,11 +432,18 @@ def tile_encoderblock_pb_t_kernel(tc, h, W1, b1, W2, b2, gamma2, beta2, out):
                 minus_mean_of(c)
             if live(c + 2):
                 turn_h(c + 2)
+            for i in range(SUB):
+                if by_tensor(c - 1, i):
+                    spread_finish(c - 1, i)
+                    finish_by_scalar(c - 1, i)
             if c == N_CHUNKS - 1:
                 for i in reversed(range(SUB)):
                     centre_and_scale(c, i)
             if live(c):
                 inv_deviation_of(c)
+                for i in range(SUB):
+                    if by_tensor(c, i):
+                        make_diagonal(c, i)
             if live(c + 1):
                 regroup_f1(c + 1, nc.vector.tensor_copy, slice(0, VECTOR_COLS))
                 quantise_f1(c + 1)

@@ -166,10 +166,22 @@ def tile_encoderblock_pb_t_kernel(tc, h, W1, b1, W2, b2, gamma2, beta2, out):
             )
             h_quantised[c] = (h_codes, h_scales)
 
+        def residual_of(c):
+            if c not in residuals:
+                residual = work.tile([P, SUB, D], F32, tag="gate", bufs=3)
+                residuals[c] = residual
+            return residuals[c]
+
         def add_b2_to_h(engine, c, i):
-            residual = work.tile([P, D], F32, tag="row%d" % i, bufs=3)
-            engine.tensor_tensor(out=residual[:], in0=h_all[:, c, i, :], in1=b2_all[:], op=ALU.add)
-            residuals[c, i] = residual
+            engine.tensor_tensor(
+                out=residual_of(c)[:, i, :], in0=h_all[:, c, i, :], in1=b2_all[:], op=ALU.add
+            )
+
+        def add_b2_to_chunk(c):
+            nc.gpsimd.tensor_tensor(
+                out=residual_of(c)[:], in0=h_all[:, c],
+                in1=b2_all[:].unsqueeze(1).to_broadcast([P, SUB, D]), op=ALU.add,
+            )
 
         def spread_residual(c, i):
             sum_bank = banks.tile([P, D], F32, tag="bank", bufs=7)
@@ -179,9 +191,7 @@ def tile_encoderblock_pb_t_kernel(tc, h, W1, b1, W2, b2, gamma2, beta2, out):
             nc.tensor.matmul(
                 out=sum_bank[:], lhsT=ones[:], rhs=vector_rows[:, 0, :], start=False, stop=True
             )
-            residual = work.tile([P, D], F32, tag="row%d" % i, bufs=3)
-            nc.scalar.copy(out=residual[:], in_=sum_bank[:])
-            residuals[c, i] = residual
+            nc.scalar.copy(out=residual_of(c)[:, i, :], in_=sum_bank[:])
 
         def open_f1(c):
             f1_planes_of[c] = work.tile([P, F_TILES, CHUNK], BF16, name="f1_planes")
@@ -257,9 +267,14 @@ def tile_encoderblock_pb_t_kernel(tc, h, W1, b1, W2, b2, gamma2, beta2, out):
                     start=(g == 0),
                     stop=(g == PASSES2 - 1),
                 )
-            u = work.tile([P, D], F32, tag="row%d" % i, bufs=3)
+            if i == 0:
+                wide = work.tile([P, SUB, D], F32, tag="gate", bufs=3)
+                u = wide[:, 0, :]
+            else:
+                narrow = work.tile([P, D], F32, tag="u", bufs=2 * (SUB - 1))
+                u = narrow[:]
             nc.vector.scalar_tensor_tensor(
-                out=u[:], in0=residuals[c, i][:], scalar=1.0, in1=acc2[:],
+                out=u, in0=residuals[c][:, i, :], scalar=1.0, in1=acc2[:],
                 op0=ALU.mult, op1=ALU.add, accum_out=sums_of[c]["u_sum"][:, i : i + 1],
             )
             u_of[c].append(u)
@@ -275,13 +290,13 @@ def tile_encoderblock_pb_t_kernel(tc, h, W1, b1, W2, b2, gamma2, beta2, out):
             if i in lent_tiles(c):
                 centred = work.tile([P, D], F32, bufs=SUB)
                 nc.scalar.activation(
-                    out=centred[:], in_=u_of[c][i][:], func=ACT.Identity,
+                    out=centred[:], in_=u_of[c][i], func=ACT.Identity,
                     bias=sums_of[c]["minus_mean"][:, i : i + 1], scale=1.0,
                 )
                 nc.gpsimd.tensor_tensor(out=scaled[:], in0=centred[:], in1=gamma_sb[:], op=ALU.mult)
                 return
             nc.vector.scalar_tensor_tensor(
-                out=scaled[:], in0=u_of[c][i][:], scalar=sums_of[c]["minus_mean"][:, i : i + 1],
+                out=scaled[:], in0=u_of[c][i], scalar=sums_of[c]["minus_mean"][:, i : i + 1],
                 in1=gamma_all, op0=ALU.add, op1=ALU.mult,
             )
 
@@ -291,7 +306,7 @@ def tile_encoderblock_pb_t_kernel(tc, h, W1, b1, W2, b2, gamma2, beta2, out):
             for i in range(SUB):
                 squares = work.tile([P, D], BF16, bufs=SUB)
                 nc.scalar.activation(
-                    out=squares[:], in_=u_of[c][i][:], func=ACT.Square,
+                    out=squares[:], in_=u_of[c][i], func=ACT.Square,
                     bias=minus_mean[:, i : i + 1], scale=1.0, accum_out=square_sum[:, i : i + 1],
                 )
             inv_deviation = work.tile([P, SUB], F32)
@@ -424,8 +439,7 @@ def tile_encoderblock_pb_t_kernel(tc, h, W1, b1, W2, b2, gamma2, beta2, out):
                     if not by_tensor(c - 1, i):
                         finish(c - 1, i)
             if c > 0 and live(c + 1):
-                for i in range(SUB):
-                    add_b2_to_h(nc.gpsimd, c + 1, i)
+                add_b2_to_chunk(c + 1)
             if live(c + 1):
                 regroup_f1(c + 1, nc.scalar.copy, slice(VECTOR_COLS, CHUNK))
             if live(c) and c != N_CHUNKS - 1:

from contextlib import ExitStack

import concourse.mybir as mybir
from concourse.masks import make_identity

F32 = mybir.dt.float32
BF16 = mybir.dt.bfloat16
U32 = mybir.dt.uint32
U8 = mybir.dt.uint8
FP8X4 = mybir.dt.float8_e4m3fn_x4
ACT = mybir.ActivationFunctionType
ALU = mybir.AluOpType

P = 128
PACK = 4
D = 512
F = 1024
TOKENS = 4 * 1024
SUB = 4
CHUNK = SUB * P
N_CHUNKS = TOKENS // CHUNK
F_TILES = F // P
PASSES2 = F // (P * PACK)
EPS = 1e-14
VECTOR_COLS = 448
KEPT_BACK = 2

FLOPS = 2 * TOKENS * D * F * 2


def regroup(engine_copy, grouped, planes):
    engine_copy(
        out=grouped.rearrange("p (c i) t -> p c t i", i=4),
        in_=planes.rearrange("p t (c i) -> p c t i", i=4),
    )


def tile_encoderblock_pb_t_kernel(tc, h, W1, b1, W2, b2, gamma2, beta2, out):
    nc = tc.nc
    h_chunks = h.flatten_outer_dims().rearrange("(c p i) d -> c p i d", p=P, i=SUB)
    out_chunks = out.flatten_outer_dims().rearrange("(c p i) d -> c p i d", p=P, i=SUB)

    with ExitStack() as ctx:
        ctx.enter_context(tc.manual_schedule())
        keep = ctx.enter_context(tc.tile_pool(name="keep", bufs=1))
        work = ctx.enter_context(tc.tile_pool(name="work", bufs=2))
        fixed_banks = ctx.enter_context(tc.psum_pool(name="fixed_banks", bufs=1))
        banks = ctx.enter_context(tc.psum_pool(name="banks", bufs=2))

        w1_raw = keep.tile([P, PACK, F], BF16)
        w1_rows = W1.rearrange("(u q e) f -> u q e f", u=2, e=2)
        h_all = keep.tile([P, N_CHUNKS, SUB, D], BF16)

        def load_w1_half(half):
            cols = slice(half * (F // 2), (half + 1) * (F // 2))
            for u in range(2):
                nc.sync.dma_start(out=w1_raw[:, 2 * u : 2 * u + 2, cols], in_=w1_rows[u][:, :, cols])

        for half in range(2):
            pair = slice(2 * half, 2 * half + 2)
            nc.sync.dma_start(out=h_all[:, 0, pair], in_=h_chunks[0][:, pair])
        load_w1_half(0)
        load_w1_half(1)
        w2_raw = keep.tile([P, PASSES2, PACK, D], BF16)
        nc.sync.dma_start(
            out=w2_raw[:].rearrange("p g t n -> p (g t) n"),
            in_=W2.rearrange("(m p) n -> p m n", p=P),
        )
        for c in range(1, N_CHUNKS):
            nc.sync.dma_start(out=h_all[:, c], in_=h_chunks[c])

        b1_rows = keep.tile([P, P], BF16)
        nc.vector.memset(b1_rows[:].bitcast(U32), 0)
        nc.scalar.dma_start(out=b1_rows[0:F_TILES, :], in_=b1.rearrange("(m p) -> m p", p=P))
        vector_rows = keep.tile([P, 3, D], BF16)
        nc.vector.memset(vector_rows[:].rearrange("p j n -> p (j n)").bitcast(U32), 0)
        for j, vector in enumerate((b2, gamma2, beta2)):
            nc.scalar.dma_start(out=vector_rows[0:1, j, :], in_=vector.unsqueeze(0))
        ones = keep.tile([P, P], BF16)
        nc.vector.memset(ones[:], 1.0)
        eps = keep.tile([P, 1], F32)
        nc.vector.memset(eps[:], EPS)
        identity = keep.tile([P, P], F32)
        make_identity(nc, identity[:])
        identity_bf16 = keep.tile([P, P], BF16)
        make_identity(nc, identity_bf16[:])

        b1_cols = keep.tile([P, F_TILES], F32)
        b2_all = keep.tile([P, D], F32)
        norm_bank = fixed_banks.tile([P, 2, D], BF16)
        gamma_all = norm_bank[:, 0, :]
        beta_all = norm_bank[:, 1, :]

        w1_grouped = keep.tile([P, F, PACK], BF16, align_bytes=64)
        w1_codes = keep.tile([P, F], U32, align_bytes=64)
        w1_scales = keep.tile([P, F], U8, align_bytes=64)
        w2_grouped = keep.tile([P, PASSES2, D, PACK], BF16, align_bytes=64)
        w2_codes = keep.tile([P, PASSES2, D], U32, align_bytes=64)
        w2_scales = keep.tile([P, PASSES2, D], U8, align_bytes=64)

        def regroup_w1_half(half):
            cols = slice(half * (F // 2), (half + 1) * (F // 2))
            regroup(nc.vector.tensor_copy, w1_grouped[:, cols, :], w1_raw[:, :, cols])

        def quantise_w1_half(half):
            cols = slice(half * (F // 2), (half + 1) * (F // 2))
            nc.vector.quantize_mx(
                out=w1_codes[:, cols].bitcast(FP8X4),
                scales=w1_scales[:, cols],
                in_=w1_grouped[:, cols, :].rearrange("p f t -> p (f t)"),
            )

        def prepare_w2():
            for g in range(PASSES2):
                regroup(nc.vector.tensor_copy, w2_grouped[:, g], w2_raw[:, g])
            for g in range(PASSES2):
                nc.vector.quantize_mx(
                    out=w2_codes[:, g, :].bitcast(FP8X4),
                    scales=w2_scales[:, g, :],
                    in_=w2_grouped[:, g].rearrange("p n t -> p (n t)"),
                )


        h_grouped_of = {}
        h_quantised = {}
        residuals = {}
        f1_planes_of = {}
        f1_grouped_of = {}
        f1_quantised = {}
        u_of = {}
        sums_of = {}
        scaled_of = {}
        acc1_of = {}
        finish_bank_of = {}
        done_of = {}
        diagonal_of = {}
        results_of = {}

        def turn_h(c):
            h_grouped = work.tile([P, CHUNK, PACK], BF16, align_bytes=64)
            grouped_words = h_grouped[:].rearrange("p w t -> p (w t)").bitcast(F32)
            for pair in range(SUB // 2):
                turned = banks.tile([P, 2, 2, P], F32, tag="bank", bufs=7)
                for j in range(2):
                    words = h_all[:, c, 2 * pair + j, :].bitcast(F32)
                    for u in range(2):
                        nc.tensor.transpose(
                            turned[:, j, u, :], words[:, u * P : (u + 1) * P], identity[:]
                        )
                nc.scalar.copy(
                    out=grouped_words[:, pair * 4 * P : (pair + 1) * 4 * P].rearrange(
                        "p (j r u) -> p j r u", j=2, u=2
                    ),
                    in_=turned[:].rearrange("p j u r -> p j r u"),
                )
            h_grouped_of[c] = h_grouped

        def quantise_h(c):
            h_grouped = h_grouped_of.pop(c)
            h_codes = work.tile([P, CHUNK], U32, align_bytes=64)
            h_scales = work.tile([P, CHUNK], U8, align_bytes=64)
            nc.vector.quantize_mx(
                out=h_codes[:].bitcast(FP8X4),
                scales=h_scales[:],
                in_=h_grouped[:].rearrange("p w t -> p (w t)"),
            )
            h_quantised[c] = (h_codes, h_scales)

        def residual_of(c):
            if c not in residuals:
                residual = work.tile([P, SUB, D], F32, tag="gate", bufs=3)
                residuals[c] = residual
            return residuals[c]

        def add_b2_to_h(engine, c, i):
            engine.tensor_tensor(
                out=residual_of(c)[:, i, :], in0=h_all[:, c, i, :], in1=b2_all[:], op=ALU.add
            )

        def add_b2_to_chunk(c):
            nc.gpsimd.tensor_tensor(
                out=residual_of(c)[:], in0=h_all[:, c],
                in1=b2_all[:].unsqueeze(1).to_broadcast([P, SUB, D]), op=ALU.add,
            )

        def spread_residual(c, i):
            sum_bank = banks.tile([P, D], F32, tag="bank", bufs=7)
            nc.tensor.matmul(
                out=sum_bank[:], lhsT=identity_bf16[:], rhs=h_all[:, c, i, :], start=True, stop=False
            )
            nc.tensor.matmul(
                out=sum_bank[:], lhsT=ones[:], rhs=vector_rows[:, 0, :], start=False, stop=True
            )
            nc.scalar.copy(out=residual_of(c)[:, i, :], in_=sum_bank[:])

        def open_f1(c):
            f1_planes_of[c] = work.tile([P, F_TILES, CHUNK], BF16, name="f1_planes")
            f1_grouped_of[c] = work.tile(
                [P, PASSES2, CHUNK, PACK], BF16, name="f1_grouped", align_bytes=64
            )

        def first_matmul(c, m):
            h_codes, h_scales = h_quantised[c]
            units = slice(m * P, (m + 1) * P)
            acc1 = banks.tile([P, CHUNK], F32, tag="bank", bufs=7)
            nc.tensor.matmul_mx(
                out=acc1[:],
                lhsT=w1_codes[:, units].bitcast(FP8X4),
                lhsT_scale=w1_scales[:, units],
                rhs=h_codes[:].bitcast(FP8X4),
                rhs_scale=h_scales[:],
                start=True,
                stop=True,
            )
            acc1_of[c, m] = acc1

        def add_b1(c, m, by_vector=False):
            bank = acc1_of.pop((c, m))
            bias = b1_cols[:, m : m + 1]
            if by_vector:
                nc.vector.tensor_scalar(
                    out=f1_planes_of[c][:, m, :], in0=bank[:], scalar1=bias, scalar2=None, op0=ALU.add
                )
            else:
                nc.scalar.activation(
                    out=f1_planes_of[c][:, m, :], in_=bank[:], func=ACT.Identity, bias=bias, scale=1.0
                )

        def regroup_f1(c, engine_copy, cols, passes=range(PASSES2)):
            for g in passes:
                regroup(
                    engine_copy,
                    f1_grouped_of[c][:, g, cols, :],
                    f1_planes_of[c][:, g * PACK : (g + 1) * PACK, cols],
                )

        def quantise_f1(c, passes=range(PASSES2)):
            f1_grouped = f1_grouped_of[c]
            if c not in f1_quantised:
                f1_codes = work.tile([P, PASSES2, CHUNK], U32, align_bytes=64)
                f1_scales = work.tile([P, PASSES2, CHUNK], U8, align_bytes=64)
                f1_quantised[c] = (f1_codes, f1_scales)
            f1_codes, f1_scales = f1_quantised[c]
            for g in passes:
                nc.vector.quantize_mx(
                    out=f1_codes[:, g, :].bitcast(FP8X4),
                    scales=f1_scales[:, g, :],
                    in_=f1_grouped[:, g].rearrange("p w t -> p (w t)"),
                )

        def open_u(c):
            u_of[c] = []
            scaled_of[c] = {}
            sums_of[c] = {"u_sum": work.tile([P, SUB], F32, name="u_sum")}

        def second_matmul(c, i):
            f1_codes, f1_scales = f1_quantised[c]
            tokens = slice(i * P, (i + 1) * P)
            acc2 = banks.tile([P, D], F32, tag="bank", bufs=7)
            for g in range(PASSES2):
                nc.tensor.matmul_mx(
                    out=acc2[:],
                    lhsT=f1_codes[:, g, tokens].bitcast(FP8X4),
                    lhsT_scale=f1_scales[:, g, tokens],
                    rhs=w2_codes[:, g, :].bitcast(FP8X4),
                    rhs_scale=w2_scales[:, g, :],
                    start=(g == 0),
                    stop=(g == PASSES2 - 1),
                )
            if i == 0:
                wide = work.tile([P, SUB, D], F32, tag="gate", bufs=3)
                u = wide[:, 0, :]
            else:
                narrow = work.tile([P, D], F32, tag="u", bufs=2 * (SUB - 1))
                u = narrow[:]
            nc.vector.scalar_tensor_tensor(
                out=u, in0=residuals[c][:, i, :], scalar=1.0, in1=acc2[:],
                op0=ALU.mult, op1=ALU.add, accum_out=sums_of[c]["u_sum"][:, i : i + 1],
            )
            u_of[c].append(u)

        def minus_mean_of(c):
            minus_mean = work.tile([P, SUB], F32)
            nc.scalar.mul(out=minus_mean[:], in_=sums_of[c]["u_sum"][:], mul=-1.0 / D)
            sums_of[c]["minus_mean"] = minus_mean

        def centre_and_scale(c, i):
            scaled = work.tile([P, D], F32, bufs=2 * SUB)
            scaled_of[c][i] = scaled
            if i in lent_tiles(c):
                centred = work.tile([P, D], F32, bufs=SUB)
                nc.scalar.activation(
                    out=centred[:], in_=u_of[c][i], func=ACT.Identity,
                    bias=sums_of[c]["minus_mean"][:, i : i + 1], scale=1.0,
                )
                nc.gpsimd.tensor_tensor(out=scaled[:], in0=centred[:], in1=gamma_sb[:], op=ALU.mult)
                return
            nc.vector.scalar_tensor_tensor(
                out=scaled[:], in0=u_of[c][i], scalar=sums_of[c]["minus_mean"][:, i : i + 1],
                in1=gamma_all, op0=ALU.add, op1=ALU.mult,
            )

        def inv_deviation_of(c):
            minus_mean = sums_of[c]["minus_mean"]
            square_sum = work.tile([P, SUB], F32)
            for i in range(SUB):
                squares = work.tile([P, D], BF16, bufs=SUB)
                nc.scalar.activation(
                    out=squares[:], in_=u_of[c][i], func=ACT.Square,
                    bias=minus_mean[:, i : i + 1], scale=1.0, accum_out=square_sum[:, i : i + 1],
                )
            inv_deviation = work.tile([P, SUB], F32)
            nc.scalar.activation(
                out=inv_deviation[:], in_=square_sum[:], func=ACT.Abs_reciprocal_sqrt,
                bias=eps[:], scale=1.0 / D,
            )
            sums_of[c]["inv_deviation"] = inv_deviation

        def open_result(c, i):
            if (c, i // 2) not in results_of:
                results_of[c, i // 2] = work.tile([P, 2, D], F32, name="result", bufs=4)

        def store(c, i):
            if c == N_CHUNKS - 1:
                nc.sync.dma_start(out=out_chunks[c][:, i], in_=results_of[c, i // 2][:, i % 2, :])
            else:
                done_of.setdefault((c, i // 2), []).append(i)
                if len(done_of[c, i // 2]) == 2:
                    j = i // 2 * 2
                    nc.sync.dma_start(out=out_chunks[c][:, j : j + 2], in_=results_of[c, i // 2][:])

        def make_diagonal(c, i):
            diagonal = work.tile([P, P], F32, bufs=4)
            nc.scalar.activation(
                out=diagonal[:], in_=identity[:], func=ACT.Copy,
                scale=sums_of[c]["inv_deviation"][:, i : i + 1],
            )
            diagonal_of[c, i] = diagonal

        def spread_finish(c, i):
            diagonal = diagonal_of.pop((c, i))
            finish_bank = banks.tile([P, D], F32, tag="bank", bufs=7)
            nc.tensor.matmul(
                out=finish_bank[:], lhsT=diagonal[:], rhs=scaled_of[c][i][:], start=True, stop=False
            )
            nc.tensor.matmul(
                out=finish_bank[:], lhsT=ones[:], rhs=vector_rows[:, 2, :], start=False, stop=True
            )
            finish_bank_of[c] = finish_bank

        def finish_by_scalar(c, i):
            open_result(c, i)
            nc.scalar.copy(out=results_of[c, i // 2][:, i % 2, :], in_=finish_bank_of.pop(c)[:])
            store(c, i)

        def by_tensor(c, i):
            return i in (0,) and 0 <= c <= 5

        def finish(c, i):
            open_result(c, i)
            nc.vector.scalar_tensor_tensor(
                out=results_of[c, i // 2][:, i % 2, :], in0=scaled_of[c][i][:],
                scalar=sums_of[c]["inv_deviation"][:, i : i + 1],
                in1=beta_all, op0=ALU.mult, op1=ALU.add,
            )
            store(c, i)

        def lent_tiles(c):
            return (2, 3) if c == N_CHUNKS - 2 else (3,) if c == N_CHUNKS - 1 else ()

        def live(c):
            return 0 <= c < N_CHUNKS

        b1_rows_f32 = keep.tile([P, P], F32)
        b1_turned = banks.tile([P, D], F32, tag="bank", bufs=7)
        b2_bank = banks.tile([P, D], F32, tag="bank", bufs=7)
        turn_h(0)
        regroup_w1_half(0)
        quantise_h(0)
        quantise_w1_half(0)
        nc.scalar.copy(out=b1_rows_f32[:], in_=b1_rows[:])
        nc.tensor.transpose(b1_turned[:, 0:P], b1_rows_f32[:], identity[:])
        nc.tensor.matmul(out=b2_bank[:], lhsT=ones[:], rhs=vector_rows[:, 0, :], start=True, stop=True)
        nc.scalar.copy(out=b1_cols[:], in_=b1_turned[:, 0:F_TILES])
        nc.scalar.copy(out=b2_all[:], in_=b2_bank[:])
        regroup_w1_half(1)
        quantise_w1_half(1)
        open_f1(0)
        for m in range(F_TILES):
            if m == 4:
                turn_h(1)
            first_matmul(0, m)
            if m not in (7,):
                add_b1(0, m)
        for j, spread in enumerate((gamma_all, beta_all)):
            nc.tensor.matmul(out=spread, lhsT=ones[:], rhs=vector_rows[:, 1 + j, :], start=True, stop=True)
        gamma_sb = keep.tile([P, D], BF16)
        for i in range(SUB):
            spread_residual(0, i)
        nc.scalar.copy(out=gamma_sb[:], in_=gamma_all)
        prepare_w2()
        regroup_f1(0, nc.vector.tensor_copy, slice(0, CHUNK), (0,))
        quantise_f1(0, (0,))
        quantise_h(1)
        open_f1(1)
        for m in range(2):
            first_matmul(1, m)
            add_b1(1, m)
        add_b1(0, 7, by_vector=True)
        regroup_f1(0, nc.vector.tensor_copy, slice(0, CHUNK), (1,))
        quantise_f1(0, (1,))

        for c in range(N_CHUNKS + 1):
            if 0 < c < N_CHUNKS:
                for i in range(SUB):
                    centre_and_scale(c - 1, i)
            if live(c):
                open_u(c)
            if c > 0 and live(c + 1):
                open_f1(c + 1)
            tiles = list(range(2 if c == 0 else 0, F_TILES)) if live(c + 1) else []
            for i in range(SUB):
                mine = tiles[len(tiles) * i // SUB : len(tiles) * (i + 1) // SUB]
                if live(c):
                    second_matmul(c, i)
                for m in mine[:1]:
                    first_matmul(c + 1, m)
                    add_b1(c + 1, m)
                if live(c - 1) and c != N_CHUNKS - 1 and not by_tensor(c - 1, i):
                    finish(c - 1, i)
                if c == 0:
                    add_b2_to_h(nc.vector, 1, i)
                for m in mine[1:]:
                    first_matmul(c + 1, m)
                    add_b1(c + 1, m)
            if c == N_CHUNKS - 1:
                minus_mean_of(c)
                for i in range(SUB):
                    if not by_tensor(c - 1, i):
                        finish(c - 1, i)
            if c > 0 and live(c + 1):
                add_b2_to_chunk(c + 1)
            if live(c + 1):
                regroup_f1(c + 1, nc.scalar.copy, slice(VECTOR_COLS, CHUNK))
            if live(c) and c != N_CHUNKS - 1:
                minus_mean_of(c)
            if live(c + 2):
                turn_h(c + 2)
            for i in range(SUB):
                if by_tensor(c - 1, i):
                    spread_finish(c - 1, i)
                    finish_by_scalar(c - 1, i)
            if c == N_CHUNKS - 1:
                for i in reversed(range(SUB)):
                    centre_and_scale(c, i)
            if live(c):
                inv_deviation_of(c)
                for i in range(SUB):
                    if by_tensor(c, i):
                        make_diagonal(c, i)
            if live(c + 1):
                regroup_f1(c + 1, nc.vector.tensor_copy, slice(0, VECTOR_COLS))
                quantise_f1(c + 1)
            if live(c + 2):
                quantise_h(c + 2)
